import numpy as np
import ml_dtypes


def mxq(x, axis, fmt="e4m3"):
    dtype, down = {"e4m3": (ml_dtypes.float8_e4m3fn, 7), "e5m2": (ml_dtypes.float8_e5m2, 14)}[fmt]
    v = np.moveaxis(np.asarray(x, np.float32).astype(ml_dtypes.bfloat16).astype(np.float64), axis, -1)
    blocks = v.reshape(v.shape[:-1] + (-1, 32))
    amax = np.abs(blocks).max(-1, keepdims=True)
    byte = np.maximum(np.where(amax > 0, np.frexp(amax)[1] - 1 + 127, 0) - down, 1)
    scale = np.exp2(byte - 127.0)
    codes = (blocks / scale).astype(np.float32).astype(dtype).astype(np.float64)
    return np.moveaxis((codes * scale).reshape(v.shape), -1, axis)


WIDE = False


def mx_kscale(k):
    if not WIDE:
        return np.ones(k)
    levels = np.array([10, -10, 5, -5, 0])
    if k % 512:
        return np.exp2(np.random.permutation(np.resize(levels, k // 32))).repeat(32)
    a = np.empty((k // 512, 16))
    for p in range(k // 512):
        a[p, :8] = np.random.permutation(np.resize(levels, 8))
        for g in range(8):
            far = levels[np.abs(levels - a[p, g]) >= 10]
            a[p, g + 8] = far[np.random.randint(len(far))]
    return np.exp2(a.ravel()).repeat(32)


BF16 = ml_dtypes.bfloat16


def bf(x):
    return np.asarray(x, np.float32).astype(BF16)


def f64(x):
    return np.asarray(x).astype(np.float64)


B, GH, GW, F_IN, F_OUT = 2, 16, 16, 16384, 512


def setup_inputs():
    s = mx_kscale(F_IN)
    return {"X": bf(np.random.standard_normal((B, GH * GW, F_IN)) * s),
            "W_gcn": bf(np.random.standard_normal((F_IN, F_OUT)) * 0.5 / np.sqrt(F_IN) / s[:, None]),
            "b": bf(np.random.standard_normal(F_OUT) * 0.3),
            "H": GH, "Wd": GW}


def _neighbor_sum(Xg):
    p = np.pad(Xg, ((0, 0), (1, 1), (1, 1), (0, 0)))
    return (p[:, :-2, 1:-1] + p[:, 2:, 1:-1]
            + p[:, 1:-1, :-2] + p[:, 1:-1, 2:])


def reference(X, W_gcn, b, H, Wd):
    X = f64(X)
    Bn, N, F = X.shape
    Xg = X.reshape(Bn, H, Wd, F)
    AX = _neighbor_sum(Xg).reshape(Bn, N, F)
    return (mxq(AX, 2, "e4m3") @ mxq(f64(W_gcn), 0, "e4m3")) + f64(b)

@@ -1,0 +1,270 @@
+from contextlib import ExitStack
+
+import concourse.masks as masks
+import concourse.mybir as mybir
+
+BF16 = mybir.dt.bfloat16
+F32 = mybir.dt.float32
+U32 = mybir.dt.uint32
+U8 = mybir.dt.uint8
+FP8X4 = mybir.dt.float8_e4m3fn_x4
+ADD = mybir.AluOpType.add
+
+P = 128
+PACK = 4
+K_PASS = P * PACK
+BATCH = 2
+GRID = 16
+NODES = BATCH * GRID * GRID
+F_IN = 16384
+F_OUT = 512
+PASSES = F_IN // K_PASS
+NODE_TILES = NODES // P
+LOADS_AHEAD = 6
+SUMS = GRID + 1
+PAIR_PITCH = (SUMS + 1) * PACK
+MID_FIRST = 64
+
+FLOPS = 2 * NODES * F_IN * F_OUT + 3 * NODES * F_IN + NODES * F_OUT
+
+
+def sums_on_tensor(g):
+    return (3 * g + 3) % 8 < 3
+
+
+def tile_graphconvlayer_k_kernel(tc, X, W_gcn, b, H, Wd, out):
+    nc = tc.nc
+    assert H == GRID and Wd == GRID
+
+    x_rows = X.rearrange("b n f -> (b n) f").rearrange("(r p) f -> p r f", p=P)
+    out_rows = out.rearrange("b n o -> (b n) o")
+
+    with ExitStack() as ctx:
+        const = ctx.enter_context(tc.tile_pool(name="const", bufs=1))
+        loads = ctx.enter_context(tc.tile_pool(name="loads", bufs=LOADS_AHEAD + 2))
+        work = ctx.enter_context(tc.tile_pool(name="work", bufs=2))
+        regrouped = ctx.enter_context(tc.tile_pool(name="regrouped", bufs=3))
+        pairs = ctx.enter_context(tc.tile_pool(name="pairs", bufs=3))
+        quant = ctx.enter_context(tc.tile_pool(name="quant", bufs=3))
+        acc_pool = ctx.enter_context(tc.psum_pool(name="acc", bufs=1))
+        xt_pool = ctx.enter_context(tc.psum_pool(name="xt", bufs=4))
+
+        ident = const.tile([P, P], F32, name="ident")
+        masks.make_identity(nc, ident[:])
+
+        bordered = [
+            const.tile([P, BATCH, SUMS, SUMS * PACK], BF16, name="bordered%d" % s) for s in range(3)
+        ]
+        for s in range(3):
+            nc.vector.memset(bordered[s][:], 0.0)
+
+        wide = const.tile([P, P + 2 * GRID], BF16, name="wide")
+        nc.vector.memset(wide[:], 0.0)
+        nc.vector.tensor_copy(out=wide[:, GRID : GRID + P], in_=ident[:])
+        adjacency = const.tile([P, P], BF16, name="adjacency")
+        nc.vector.tensor_tensor(
+            out=adjacency[:], in0=wide[:, 0:P], in1=wide[:, 2 * GRID : 2 * GRID + P], op=ADD
+        )
+        by_row = adjacency[:].rearrange("p (i j) -> p i j", j=GRID)
+        from_left = wide[:, GRID - 1 : GRID - 1 + P].rearrange("p (i j) -> p i j", j=GRID)
+        from_right = wide[:, GRID + 1 : GRID + 1 + P].rearrange("p (i j) -> p i j", j=GRID)
+        nc.vector.tensor_tensor(
+            out=by_row[:, :, 1:GRID], in0=by_row[:, :, 1:GRID], in1=from_left[:, :, 1:GRID], op=ADD
+        )
+        nc.vector.tensor_tensor(
+            out=by_row[:, :, 0 : GRID - 1],
+            in0=by_row[:, :, 0 : GRID - 1],
+            in1=from_right[:, :, 0 : GRID - 1],
+            op=ADD,
+        )
+
+        acc = [acc_pool.tile([P, F_OUT], F32, name="acc%d" % r) for r in range(NODE_TILES)]
+        bias = const.tile([P, F_OUT], BF16, name="bias")
+
+        x_pass = {}
+        x_middle = {}
+        w_pass = {}
+        pair_sums = {}
+        ax_grouped = {}
+        ax_codes = {}
+        ax_scales = {}
+        w_grouped = {}
+        w_codes = {}
+        w_scales = {}
+
+        def load(g):
+            features = slice(g * K_PASS, (g + 1) * K_PASS)
+            x_sb = loads.tile([P, NODE_TILES, K_PASS], BF16, name="x_sb")
+            nc.sync.dma_start(out=x_sb[:], in_=x_rows[:, :, features])
+            x_pass[g] = x_sb
+            if sums_on_tensor(g):
+                x_mid = loads.tile([P, BATCH, K_PASS], BF16, name="x_mid")
+                nc.sync.dma_start(
+                    out=x_mid[:],
+                    in_=X[:, MID_FIRST : MID_FIRST + P, features].rearrange("b p f -> p b f"),
+                )
+                x_middle[g] = x_mid
+            w_sb = loads.tile([P, PACK, F_OUT], BF16, name="w_sb")
+            nc.sync.dma_start(
+                out=w_sb[:],
+                in_=W_gcn[features, :].rearrange("(p t) o -> p t o", t=PACK),
+            )
+            w_pass[g] = w_sb
+
+        def transpose_x(g):
+            words = x_pass[g][:].bitcast(F32)
+            for bb in range(BATCH):
+                xt = xt_pool.tile([P, 2, GRID * GRID], F32, name="xt")
+                for u in range(2):
+                    for half in range(2):
+                        nc.tensor.transpose(
+                            xt[:, u, half * P : (half + 1) * P],
+                            words[:, 2 * bb + half, u : 2 * P : 2],
+                            ident[:],
+                        )
+                inner = bordered[g % 3][:].bitcast(F32)[:, bb, 0:GRID, 2 : 2 + 2 * GRID]
+                nc.scalar.copy(
+                    out=inner.rearrange("p i (j u) -> p i j u", u=2),
+                    in_=xt[:].rearrange("p u (i j) -> p i j u", j=GRID),
+                )
+
+        def sum_on_tensor(g):
+            grouped = work.tile([P, NODES * PACK], BF16, name="ax_plain", align_bytes=64)
+            edge = P - GRID
+            for bb in range(BATCH):
+                upper = xt_pool.tile([P, PACK, P], F32, name="xt")
+                lower = xt_pool.tile([P, PACK, P], F32, name="xt")
+                for t in range(PACK):
+                    x_up = x_pass[g][:, 2 * bb, t:K_PASS:PACK]
+                    x_mid = x_middle[g][:, bb, t:K_PASS:PACK]
+                    x_low = x_pass[g][:, 2 * bb + 1, t:K_PASS:PACK]
+                    for dst, lhsT, columns in (
+                        (upper[:, t, 0:edge], x_up, adjacency[:, 0:edge]),
+                        (upper[:, t, edge:P], x_mid, adjacency[:, 3 * GRID : 4 * GRID]),
+                        (lower[:, t, 0:GRID], x_mid, adjacency[:, 4 * GRID : 5 * GRID]),
+                        (lower[:, t, GRID:P], x_low, adjacency[:, GRID:P]),
+                    ):
+                        nc.tensor.matmul(out=dst, lhsT=lhsT, rhs=columns, start=True, stop=True)
+                for half, bank in enumerate((upper, lower)):
+                    r = 2 * bb + half
+                    nc.scalar.copy(
+                        out=grouped[:, r * P * PACK : (r + 1) * P * PACK].rearrange(
+                            "p (n t) -> p n t", t=PACK
+                        ),
+                        in_=bank[:].rearrange("p t n -> p n t"),
+                    )
+            ax_grouped[g] = grouped[:]
+
+        def regroup_w(g):
+            rows = w_pass[g][:]
+            grouped = regrouped.tile([P, F_OUT, PACK], BF16, name="w_grouped", align_bytes=64)
+            nc.scalar.copy(
+                out=grouped[:].rearrange("p (c i) t -> p c t i", i=4),
+                in_=rows.rearrange("p t (c i) -> p c t i", i=4),
+            )
+            w_grouped[g] = grouped
+
+        def quantise_w(g):
+            codes = quant.tile([P, F_OUT], U32, name="w_codes", align_bytes=64)
+            scales = quant.tile([P, F_OUT], U8, name="w_scales", align_bytes=64)
+            nc.vector.quantize_mx(
+                out=codes[:].bitcast(FP8X4),
+                scales=scales[:],
+                in_=w_grouped[g][:].rearrange("p o t -> p (o t)"),
+            )
+            w_codes[g] = codes
+            w_scales[g] = scales
+
+        def copy_single_terms(g):
+            src = bordered[g % 3]
+            inner = GRID * PACK
+            pair = pairs.tile([P, BATCH, SUMS, PAIR_PITCH], F32, name="pair")
+            nc.scalar.copy(out=pair[:, :, 0, 0 : SUMS * PACK], in_=src[:, :, 0, :])
+            nc.scalar.copy(
+                out=pair[:, :, 1:SUMS, inner : inner + PACK], in_=src[:, :, 1:SUMS, inner : inner + PACK]
+            )
+            pair_sums[g] = pair
+
+        def add_pairs(g):
+            src = bordered[g % 3]
+            inner = GRID * PACK
+            nc.vector.tensor_tensor(
+                out=pair_sums[g][:, :, 1:SUMS, 0:inner],
+                in0=src[:, :, 0:GRID, PACK : PACK + inner],
+                in1=src[:, :, 1:SUMS, 0:inner],
+                op=ADD,
+            )
+
+        def add_sums(g):
+            pair = pair_sums[g]
+            grouped = work.tile([P, BATCH, GRID, GRID * PACK], BF16, name="ax_grouped", align_bytes=64)
+            nc.vector.tensor_tensor(
+                out=grouped[:],
+                in0=pair[:, :, 0:GRID, 0 : GRID * PACK],
+                in1=pair[:, :, 1 : 1 + GRID, PACK : PACK + GRID * PACK],
+                op=ADD,
+            )
+            ax_grouped[g] = grouped[:].rearrange("p b i c -> p (b i c)")
+
+        def quantise_ax(g):
+            codes = quant.tile([P, NODES], U32, name="ax_codes", align_bytes=64)
+            scales = quant.tile([P, NODES], U8, name="ax_scales", align_bytes=64)
+            nc.vector.quantize_mx(
+                out=codes[:].bitcast(FP8X4),
+                scales=scales[:],
+                in_=ax_grouped[g],
+            )
+            ax_codes[g] = codes
+            ax_scales[g] = scales
+
+        def multiply(g):
+            for r in range(NODE_TILES):
+                nodes = slice(r * P, (r + 1) * P)
+                nc.tensor.matmul_mx(
+                    out=acc[r][:],
+                    lhsT=ax_codes[g][:, nodes].bitcast(FP8X4),
+                    lhsT_scale=ax_scales[g][:, nodes],
+                    rhs=w_codes[g][:].bitcast(FP8X4),
+                    rhs_scale=w_scales[g][:],
+                    start=(g == 0),
+                    stop=(g == PASSES - 1),
+                )
+
+        def prepare(g):
+            if g + LOADS_AHEAD < PASSES:
+                load(g + LOADS_AHEAD)
+            if sums_on_tensor(g):
+                regroup_w(g)
+                sum_on_tensor(g)
+            else:
+                transpose_x(g)
+                regroup_w(g)
+                copy_single_terms(g)
+
+        with tc.manual_schedule():
+            for g in range(LOADS_AHEAD):
+                load(g)
+            prepare(0)
+            add_pairs(0)
+            quantise_w(0)
+            prepare(1)
+            nc.sync.dma_start(out=bias[:], in_=b.partition_broadcast(P))
+            for g in range(PASSES):
+                if g + 2 < PASSES:
+                    prepare(g + 2)
+                if not sums_on_tensor(g):
+                    add_sums(g)
+                if g >= 1:
+                    quantise_ax(g - 1)
+                    multiply(g - 1)
+                if g + 1 < PASSES:
+                    if not sums_on_tensor(g + 1):
+                        add_pairs(g + 1)
+                    quantise_w(g + 1)
+            quantise_ax(PASSES - 1)
+            multiply(PASSES - 1)
+
+            for r in range(NODE_TILES):
+                result = work.tile([P, F_OUT], F32, name="result")
+                nc.vector.tensor_tensor(out=result[:], in0=acc[r][:], in1=bias[:], op=ADD)
+                nc.sync.dma_start(out=out_rows[r * P : (r + 1) * P, :], in_=result[:])

@@ -46,6 +46,7 @@ def tile_graphconvlayer_k_kernel(tc, X, W_gcn, b, H, Wd, out):
         regrouped = ctx.enter_context(tc.tile_pool(name="regrouped", bufs=3))
         pairs = ctx.enter_context(tc.tile_pool(name="pairs", bufs=3))
         quant = ctx.enter_context(tc.tile_pool(name="quant", bufs=3))
+        results = ctx.enter_context(tc.tile_pool(name="results", bufs=NODE_TILES))
         acc_pool = ctx.enter_context(tc.psum_pool(name="acc", bufs=1))
         xt_pool = ctx.enter_context(tc.psum_pool(name="xt", bufs=4))
 
@@ -56,7 +57,8 @@ def tile_graphconvlayer_k_kernel(tc, X, W_gcn, b, H, Wd, out):
             const.tile([P, BATCH, SUMS, SUMS * PACK], BF16, name="bordered%d" % s) for s in range(3)
         ]
         for s in range(3):
-            nc.vector.memset(bordered[s][:], 0.0)
+            nc.gpsimd.memset(bordered[s][:, :, GRID, :], 0.0)
+            nc.gpsimd.memset(bordered[s][:, :, 0:GRID, 0:PACK], 0.0)
 
         wide = const.tile([P, P + 2 * GRID], BF16, name="wide")
         nc.vector.memset(wide[:], 0.0)
@@ -129,31 +131,22 @@ def tile_graphconvlayer_k_kernel(tc, X, W_gcn, b, H, Wd, out):
                 )
 
         def sum_on_tensor(g):
-            grouped = work.tile([P, NODES * PACK], BF16, name="ax_plain", align_bytes=64)
+            grouped = work.tile([P, BATCH, GRID * GRID, PACK], BF16, name="ax_plain", align_bytes=64)
             edge = P - GRID
             for bb in range(BATCH):
-                upper = xt_pool.tile([P, PACK, P], F32, name="xt")
-                lower = xt_pool.tile([P, PACK, P], F32, name="xt")
+                bank = xt_pool.tile([P, PACK, GRID * GRID], BF16, name="xt")
                 for t in range(PACK):
                     x_up = x_pass[g][:, 2 * bb, t:K_PASS:PACK]
                     x_mid = x_middle[g][:, bb, t:K_PASS:PACK]
                     x_low = x_pass[g][:, 2 * bb + 1, t:K_PASS:PACK]
                     for dst, lhsT, columns in (
-                        (upper[:, t, 0:edge], x_up, adjacency[:, 0:edge]),
-                        (upper[:, t, edge:P], x_mid, adjacency[:, 3 * GRID : 4 * GRID]),
-                        (lower[:, t, 0:GRID], x_mid, adjacency[:, 4 * GRID : 5 * GRID]),
-                        (lower[:, t, GRID:P], x_low, adjacency[:, GRID:P]),
+                        (bank[:, t, 0:edge], x_up, adjacency[:, 0:edge]),
+                        (bank[:, t, edge : P + GRID], x_mid, adjacency[:, 3 * GRID : 5 * GRID]),
+                        (bank[:, t, P + GRID :], x_low, adjacency[:, GRID:P]),
                     ):
                         nc.tensor.matmul(out=dst, lhsT=lhsT, rhs=columns, start=True, stop=True)
-                for half, bank in enumerate((upper, lower)):
-                    r = 2 * bb + half
-                    nc.scalar.copy(
-                        out=grouped[:, r * P * PACK : (r + 1) * P * PACK].rearrange(
-                            "p (n t) -> p n t", t=PACK
-                        ),
-                        in_=bank[:].rearrange("p t n -> p n t"),
-                    )
-            ax_grouped[g] = grouped[:]
+                nc.scalar.copy(out=grouped[:, bb], in_=bank[:].rearrange("p t n -> p n t"))
+            ax_grouped[g] = grouped[:].rearrange("p b n t -> p (b n t)")
 
         def regroup_w(g):
             rows = w_pass[g][:]
@@ -265,6 +258,6 @@ def tile_graphconvlayer_k_kernel(tc, X, W_gcn, b, H, Wd, out):
             multiply(PASSES - 1)
 
             for r in range(NODE_TILES):
-                result = work.tile([P, F_OUT], F32, name="result")
+                result = results.tile([P, F_OUT], F32, name="result")
                 nc.vector.tensor_tensor(out=result[:], in0=acc[r][:], in1=bias[:], op=ADD)
                 nc.sync.dma_start(out=out_rows[r * P : (r + 1) * P, :], in_=result[:])

@@ -21,8 +21,10 @@ F_OUT = 512
 PASSES = F_IN // K_PASS
 NODE_TILES = NODES // P
 LOADS_AHEAD = 6
+LINE = GRID * PACK
 SUMS = GRID + 1
 PAIR_PITCH = (SUMS + 1) * PACK
+PAIR_TILES = 3
 MID_FIRST = 64
 
 FLOPS = 2 * NODES * F_IN * F_OUT + 3 * NODES * F_IN + NODES * F_OUT
@@ -30,6 +32,10 @@ FLOPS = 2 * NODES * F_IN * F_OUT + 3 * NODES * F_IN + NODES * F_OUT
 
 def sums_on_tensor(g):
     return (3 * g + 3) % 8 < 3
+
+
+def regroup_on_vector(g):
+    return g % 8 == 0
 
 
 def tile_graphconvlayer_k_kernel(tc, X, W_gcn, b, H, Wd, out):
@@ -44,7 +50,7 @@ def tile_graphconvlayer_k_kernel(tc, X, W_gcn, b, H, Wd, out):
         loads = ctx.enter_context(tc.tile_pool(name="loads", bufs=LOADS_AHEAD + 2))
         work = ctx.enter_context(tc.tile_pool(name="work", bufs=2))
         regrouped = ctx.enter_context(tc.tile_pool(name="regrouped", bufs=3))
-        pairs = ctx.enter_context(tc.tile_pool(name="pairs", bufs=3))
+        turned = ctx.enter_context(tc.tile_pool(name="turned", bufs=3))
         quant = ctx.enter_context(tc.tile_pool(name="quant", bufs=3))
         results = ctx.enter_context(tc.tile_pool(name="results", bufs=NODE_TILES))
         acc_pool = ctx.enter_context(tc.psum_pool(name="acc", bufs=1))
@@ -53,12 +59,13 @@ def tile_graphconvlayer_k_kernel(tc, X, W_gcn, b, H, Wd, out):
         ident = const.tile([P, P], F32, name="ident")
         masks.make_identity(nc, ident[:])
 
-        bordered = [
-            const.tile([P, BATCH, SUMS, SUMS * PACK], BF16, name="bordered%d" % s) for s in range(3)
+        pair_tiles = [
+            const.tile([P, BATCH, SUMS, PAIR_PITCH], F32, name="pair%d" % s)
+            for s in range(PAIR_TILES)
         ]
-        for s in range(3):
-            nc.gpsimd.memset(bordered[s][:, :, GRID, :], 0.0)
-            nc.gpsimd.memset(bordered[s][:, :, 0:GRID, 0:PACK], 0.0)
+        for s in range(PAIR_TILES):
+            nc.gpsimd.memset(pair_tiles[s][:, :, 0, 0:PACK], 0.0)
+            nc.gpsimd.memset(pair_tiles[s][:, :, GRID, LINE : LINE + PACK], 0.0)
 
         wide = const.tile([P, P + 2 * GRID], BF16, name="wide")
         nc.vector.memset(wide[:], 0.0)
@@ -86,7 +93,7 @@ def tile_graphconvlayer_k_kernel(tc, X, W_gcn, b, H, Wd, out):
         x_pass = {}
         x_middle = {}
         w_pass = {}
-        pair_sums = {}
+        x_turned = {}
         ax_grouped = {}
         ax_codes = {}
         ax_scales = {}
@@ -115,6 +122,7 @@ def tile_graphconvlayer_k_kernel(tc, X, W_gcn, b, H, Wd, out):
 
         def transpose_x(g):
             words = x_pass[g][:].bitcast(F32)
+            xt_sb = turned.tile([P, BATCH, GRID * LINE], BF16, name="xt_sb", align_bytes=64)
             for bb in range(BATCH):
                 xt = xt_pool.tile([P, 2, GRID * GRID], F32, name="xt")
                 for u in range(2):
@@ -124,11 +132,11 @@ def tile_graphconvlayer_k_kernel(tc, X, W_gcn, b, H, Wd, out):
                             words[:, 2 * bb + half, u : 2 * P : 2],
                             ident[:],
                         )
-                inner = bordered[g % 3][:].bitcast(F32)[:, bb, 0:GRID, 2 : 2 + 2 * GRID]
                 nc.scalar.copy(
-                    out=inner.rearrange("p i (j u) -> p i j u", u=2),
-                    in_=xt[:].rearrange("p u (i j) -> p i j u", j=GRID),
+                    out=xt_sb[:, bb].bitcast(F32).rearrange("p (n u) -> p n u", u=2),
+                    in_=xt[:].rearrange("p u n -> p n u"),
                 )
+            x_turned[g] = xt_sb[:].rearrange("p b (i c) -> p b i c", c=LINE)
 
         def sum_on_tensor(g):
             grouped = work.tile([P, BATCH, GRID * GRID, PACK], BF16, name="ax_plain", align_bytes=64)
@@ -151,7 +159,8 @@ def tile_graphconvlayer_k_kernel(tc, X, W_gcn, b, H, Wd, out):
         def regroup_w(g):
             rows = w_pass[g][:]
             grouped = regrouped.tile([P, F_OUT, PACK], BF16, name="w_grouped", align_bytes=64)
-            nc.scalar.copy(
+            copy = nc.vector.tensor_copy if regroup_on_vector(g) else nc.scalar.copy
+            copy(
                 out=grouped[:].rearrange("p (c i) t -> p c t i", i=4),
                 in_=rows.rearrange("p t (c i) -> p c t i", i=4),
             )
@@ -169,32 +178,32 @@ def tile_graphconvlayer_k_kernel(tc, X, W_gcn, b, H, Wd, out):
             w_scales[g] = scales
 
         def copy_single_terms(g):
-            src = bordered[g % 3]
-            inner = GRID * PACK
-            pair = pairs.tile([P, BATCH, SUMS, PAIR_PITCH], F32, name="pair")
-            nc.scalar.copy(out=pair[:, :, 0, 0 : SUMS * PACK], in_=src[:, :, 0, :])
+            src = x_turned[g]
+            pair = pair_tiles[g % PAIR_TILES]
+            nc.scalar.copy(out=pair[:, :, 0, PACK:LINE], in_=src[:, :, 0, 0 : LINE - PACK])
+            nc.scalar.copy(out=pair[:, :, GRID, PACK:LINE], in_=src[:, :, GRID - 1, PACK:LINE])
+            nc.scalar.copy(out=pair[:, :, 1:GRID, 0:PACK], in_=src[:, :, 0 : GRID - 1, 0:PACK])
             nc.scalar.copy(
-                out=pair[:, :, 1:SUMS, inner : inner + PACK], in_=src[:, :, 1:SUMS, inner : inner + PACK]
+                out=pair[:, :, 1:GRID, LINE : LINE + PACK],
+                in_=src[:, :, 1:GRID, LINE - PACK : LINE],
             )
-            pair_sums[g] = pair
 
         def add_pairs(g):
-            src = bordered[g % 3]
-            inner = GRID * PACK
+            src = x_turned[g]
             nc.vector.tensor_tensor(
-                out=pair_sums[g][:, :, 1:SUMS, 0:inner],
-                in0=src[:, :, 0:GRID, PACK : PACK + inner],
-                in1=src[:, :, 1:SUMS, 0:inner],
+                out=pair_tiles[g % PAIR_TILES][:, :, 1:GRID, PACK:LINE],
+                in0=src[:, :, 0 : GRID - 1, PACK:LINE],
+                in1=src[:, :, 1:GRID, 0 : LINE - PACK],
                 op=ADD,
             )
 
         def add_sums(g):
-            pair = pair_sums[g]
+            pair = pair_tiles[g % PAIR_TILES]
             grouped = work.tile([P, BATCH, GRID, GRID * PACK], BF16, name="ax_grouped", align_bytes=64)
             nc.vector.tensor_tensor(
                 out=grouped[:],
-                in0=pair[:, :, 0:GRID, 0 : GRID * PACK],
-                in1=pair[:, :, 1 : 1 + GRID, PACK : PACK + GRID * PACK],
+                in0=pair[:, :, 0:GRID, 0:LINE],
+                in1=pair[:, :, 1:SUMS, PACK : PACK + LINE],
                 op=ADD,
             )
             ax_grouped[g] = grouped[:].rearrange("p b i c -> p (b i c)")
@@ -227,17 +236,21 @@ def tile_graphconvlayer_k_kernel(tc, X, W_gcn, b, H, Wd, out):
             if g + LOADS_AHEAD < PASSES:
                 load(g + LOADS_AHEAD)
             if sums_on_tensor(g):
-                regroup_w(g)
+                if not regroup_on_vector(g):
+                    regroup_w(g)
                 sum_on_tensor(g)
             else:
                 transpose_x(g)
-                regroup_w(g)
+                if not regroup_on_vector(g):
+                    regroup_w(g)
                 copy_single_terms(g)
 
         with tc.manual_schedule():
             for g in range(LOADS_AHEAD):
                 load(g)
             prepare(0)
+            if regroup_on_vector(0):
+                regroup_w(0)
             add_pairs(0)
             quantise_w(0)
             prepare(1)
@@ -247,6 +260,8 @@ def tile_graphconvlayer_k_kernel(tc, X, W_gcn, b, H, Wd, out):
                     prepare(g + 2)
                 if not sums_on_tensor(g):
                     add_sums(g)
+                if g + 1 < PASSES and regroup_on_vector(g + 1):
+                    regroup_w(g + 1)
                 if g >= 1:
                     quantise_ax(g - 1)
                     multiply(g - 1)

@@ -9,6 +9,7 @@ U32 = mybir.dt.uint32
 U8 = mybir.dt.uint8
 FP8X4 = mybir.dt.float8_e4m3fn_x4
 ADD = mybir.AluOpType.add
+MULT = mybir.AluOpType.mult
 
 P = 128
 PACK = 4
@@ -20,11 +21,13 @@ F_IN = 16384
 F_OUT = 512
 PASSES = F_IN // K_PASS
 NODE_TILES = NODES // P
+POOL_COLUMNS = 256
 LOADS_AHEAD = 6
 LINE = GRID * PACK
+TOP_TO_BOTTOM = (GRID - 1) * LINE + PACK
 SUMS = GRID + 1
 PAIR_PITCH = (SUMS + 1) * PACK
-PAIR_TILES = 3
+PAIR_TILES = 4
 MID_FIRST = 64
 
 FLOPS = 2 * NODES * F_IN * F_OUT + 3 * NODES * F_IN + NODES * F_OUT
@@ -34,8 +37,12 @@ def sums_on_tensor(g):
     return (3 * g + 3) % 8 < 3
 
 
+def helped_by_pool(g):
+    return g >= 5 and not sums_on_tensor(g - 3)
+
+
 def regroup_on_vector(g):
-    return g % 8 == 0
+    return g == 0
 
 
 def tile_graphconvlayer_k_kernel(tc, X, W_gcn, b, H, Wd, out):
@@ -48,8 +55,7 @@ def tile_graphconvlayer_k_kernel(tc, X, W_gcn, b, H, Wd, out):
     with ExitStack() as ctx:
         const = ctx.enter_context(tc.tile_pool(name="const", bufs=1))
         loads = ctx.enter_context(tc.tile_pool(name="loads", bufs=LOADS_AHEAD + 2))
-        work = ctx.enter_context(tc.tile_pool(name="work", bufs=2))
-        regrouped = ctx.enter_context(tc.tile_pool(name="regrouped", bufs=3))
+        regrouped = ctx.enter_context(tc.tile_pool(name="regrouped", bufs=6))
         turned = ctx.enter_context(tc.tile_pool(name="turned", bufs=3))
         quant = ctx.enter_context(tc.tile_pool(name="quant", bufs=3))
         results = ctx.enter_context(tc.tile_pool(name="results", bufs=NODE_TILES))
@@ -94,12 +100,17 @@ def tile_graphconvlayer_k_kernel(tc, X, W_gcn, b, H, Wd, out):
         x_middle = {}
         w_pass = {}
         x_turned = {}
-        ax_grouped = {}
-        ax_codes = {}
-        ax_scales = {}
-        w_grouped = {}
-        w_codes = {}
-        w_scales = {}
+        x_psum = {}
+        grouped = {}
+        codes = {}
+        scales = {}
+
+        def values(g):
+            if g not in grouped:
+                grouped[g] = regrouped.tile(
+                    [P, NODES + F_OUT, PACK], BF16, name="mx_values", align_bytes=64
+                )
+            return grouped[g]
 
         def load(g):
             features = slice(g * K_PASS, (g + 1) * K_PASS)
@@ -120,26 +131,28 @@ def tile_graphconvlayer_k_kernel(tc, X, W_gcn, b, H, Wd, out):
             )
             w_pass[g] = w_sb
 
+        def grid(xt_sb):
+            return xt_sb[:, :, 0 : GRID * LINE].rearrange("p b (i c) -> p b i c", c=LINE)
+
         def transpose_x(g):
             words = x_pass[g][:].bitcast(F32)
-            xt_sb = turned.tile([P, BATCH, GRID * LINE], BF16, name="xt_sb", align_bytes=64)
+            xt_sb = turned.tile([P, BATCH, 2 * TOP_TO_BOTTOM], BF16, name="xt_sb", align_bytes=64)
             for bb in range(BATCH):
-                xt = xt_pool.tile([P, 2, GRID * GRID], F32, name="xt")
+                xt = xt_pool.tile([P, GRID * GRID, 2], F32, name="xt")
                 for u in range(2):
                     for half in range(2):
                         nc.tensor.transpose(
-                            xt[:, u, half * P : (half + 1) * P],
+                            xt[:, half * P : (half + 1) * P, u],
                             words[:, 2 * bb + half, u : 2 * P : 2],
                             ident[:],
                         )
-                nc.scalar.copy(
-                    out=xt_sb[:, bb].bitcast(F32).rearrange("p (n u) -> p n u", u=2),
-                    in_=xt[:].rearrange("p u n -> p n u"),
-                )
-            x_turned[g] = xt_sb[:].rearrange("p b (i c) -> p b i c", c=LINE)
+                words_out = xt[:].rearrange("p n u -> p (n u)")
+                nc.scalar.copy(out=xt_sb[:, bb, 0 : GRID * LINE].bitcast(F32), in_=words_out)
+                x_psum[g, bb] = words_out.bitcast(BF16).rearrange("p (i c) -> p i c", c=LINE)
+            x_turned[g] = xt_sb
 
         def sum_on_tensor(g):
-            grouped = work.tile([P, BATCH, GRID * GRID, PACK], BF16, name="ax_plain", align_bytes=64)
+            ax = values(g)[:, 0:NODES].rearrange("p (b n) t -> p b n t", b=BATCH)
             edge = P - GRID
             for bb in range(BATCH):
                 bank = xt_pool.tile([P, PACK, GRID * GRID], BF16, name="xt")
@@ -153,35 +166,34 @@ def tile_graphconvlayer_k_kernel(tc, X, W_gcn, b, H, Wd, out):
                         (bank[:, t, P + GRID :], x_low, adjacency[:, GRID:P]),
                     ):
                         nc.tensor.matmul(out=dst, lhsT=lhsT, rhs=columns, start=True, stop=True)
-                nc.scalar.copy(out=grouped[:, bb], in_=bank[:].rearrange("p t n -> p n t"))
-            ax_grouped[g] = grouped[:].rearrange("p b n t -> p (b n t)")
+                nc.scalar.copy(out=ax[:, bb], in_=bank[:].rearrange("p t n -> p n t"))
 
         def regroup_w(g):
-            rows = w_pass[g][:]
-            grouped = regrouped.tile([P, F_OUT, PACK], BF16, name="w_grouped", align_bytes=64)
+            first = POOL_COLUMNS if helped_by_pool(g) else 0
+            rows = w_pass[g][:, :, first:]
             copy = nc.vector.tensor_copy if regroup_on_vector(g) else nc.scalar.copy
             copy(
-                out=grouped[:].rearrange("p (c i) t -> p c t i", i=4),
+                out=values(g)[:, NODES + first :].rearrange("p (c i) t -> p c t i", i=4),
                 in_=rows.rearrange("p t (c i) -> p c t i", i=4),
             )
-            w_grouped[g] = grouped
 
-        def quantise_w(g):
-            codes = quant.tile([P, F_OUT], U32, name="w_codes", align_bytes=64)
-            scales = quant.tile([P, F_OUT], U8, name="w_scales", align_bytes=64)
-            nc.vector.quantize_mx(
-                out=codes[:].bitcast(FP8X4),
-                scales=scales[:],
-                in_=w_grouped[g][:].rearrange("p o t -> p (o t)"),
+        def regroup_w_on_pool(g):
+            nc.gpsimd.tensor_scalar(
+                out=values(g)[:, NODES : NODES + POOL_COLUMNS],
+                in0=w_pass[g][:, :, 0:POOL_COLUMNS].rearrange("p t o -> p o t"),
+                scalar1=1.0,
+                scalar2=0.0,
+                op0=MULT,
+                op1=ADD,
             )
-            w_codes[g] = codes
-            w_scales[g] = scales
 
         def copy_single_terms(g):
-            src = x_turned[g]
+            runs = x_turned[g][:].rearrange("p b (e s) -> p b e s", e=2)
+            src = grid(x_turned[g])
             pair = pair_tiles[g % PAIR_TILES]
-            nc.scalar.copy(out=pair[:, :, 0, PACK:LINE], in_=src[:, :, 0, 0 : LINE - PACK])
-            nc.scalar.copy(out=pair[:, :, GRID, PACK:LINE], in_=src[:, :, GRID - 1, PACK:LINE])
+            nc.scalar.copy(
+                out=pair[:, :, 0:SUMS:GRID, PACK:LINE], in_=runs[:, :, :, 0 : LINE - PACK]
+            )
             nc.scalar.copy(out=pair[:, :, 1:GRID, 0:PACK], in_=src[:, :, 0 : GRID - 1, 0:PACK])
             nc.scalar.copy(
                 out=pair[:, :, 1:GRID, LINE : LINE + PACK],
@@ -189,45 +201,42 @@ def tile_graphconvlayer_k_kernel(tc, X, W_gcn, b, H, Wd, out):
             )
 
         def add_pairs(g):
-            src = x_turned[g]
-            nc.vector.tensor_tensor(
-                out=pair_tiles[g % PAIR_TILES][:, :, 1:GRID, PACK:LINE],
-                in0=src[:, :, 0 : GRID - 1, PACK:LINE],
-                in1=src[:, :, 1:GRID, 0 : LINE - PACK],
-                op=ADD,
-            )
+            for bb in range(BATCH):
+                nc.vector.tensor_tensor(
+                    out=pair_tiles[g % PAIR_TILES][:, bb, 1:GRID, PACK:LINE],
+                    in0=x_psum[g, bb][:, 0 : GRID - 1, PACK:LINE],
+                    in1=grid(x_turned[g])[:, bb, 1:GRID, 0 : LINE - PACK],
+                    op=ADD,
+                )
 
         def add_sums(g):
             pair = pair_tiles[g % PAIR_TILES]
-            grouped = work.tile([P, BATCH, GRID, GRID * PACK], BF16, name="ax_grouped", align_bytes=64)
             nc.vector.tensor_tensor(
-                out=grouped[:],
+                out=values(g)[:, 0:NODES].rearrange("p (b i j) t -> p b i (j t)", b=BATCH, i=GRID),
                 in0=pair[:, :, 0:GRID, 0:LINE],
                 in1=pair[:, :, 1:SUMS, PACK : PACK + LINE],
                 op=ADD,
             )
-            ax_grouped[g] = grouped[:].rearrange("p b i c -> p (b i c)")
 
-        def quantise_ax(g):
-            codes = quant.tile([P, NODES], U32, name="ax_codes", align_bytes=64)
-            scales = quant.tile([P, NODES], U8, name="ax_scales", align_bytes=64)
+        def quantise(g, first, last):
+            if g not in codes:
+                codes[g] = quant.tile([P, NODES + F_OUT], U32, name="mx_codes", align_bytes=64)
+                scales[g] = quant.tile([P, NODES + F_OUT], U8, name="mx_scales", align_bytes=64)
             nc.vector.quantize_mx(
-                out=codes[:].bitcast(FP8X4),
-                scales=scales[:],
-                in_=ax_grouped[g],
+                out=codes[g][:, first:last].bitcast(FP8X4),
+                scales=scales[g][:, first:last],
+                in_=values(g)[:, first:last].rearrange("p n t -> p (n t)"),
             )
-            ax_codes[g] = codes
-            ax_scales[g] = scales
 
         def multiply(g):
             for r in range(NODE_TILES):
                 nodes = slice(r * P, (r + 1) * P)
                 nc.tensor.matmul_mx(
                     out=acc[r][:],
-                    lhsT=ax_codes[g][:, nodes].bitcast(FP8X4),
-                    lhsT_scale=ax_scales[g][:, nodes],
-                    rhs=w_codes[g][:].bitcast(FP8X4),
-                    rhs_scale=w_scales[g][:],
+                    lhsT=codes[g][:, nodes].bitcast(FP8X4),
+                    lhsT_scale=scales[g][:, nodes],
+                    rhs=codes[g][:, NODES:].bitcast(FP8X4),
+                    rhs_scale=scales[g][:, NODES:],
                     start=(g == 0),
                     stop=(g == PASSES - 1),
                 )
@@ -252,25 +261,29 @@ def tile_graphconvlayer_k_kernel(tc, X, W_gcn, b, H, Wd, out):
             if regroup_on_vector(0):
                 regroup_w(0)
             add_pairs(0)
-            quantise_w(0)
             prepare(1)
             nc.sync.dma_start(out=bias[:], in_=b.partition_broadcast(P))
+            prepare(2)
+            add_pairs(1)
+            add_sums(0)
+            prepare(3)
             for g in range(PASSES):
-                if g + 2 < PASSES:
-                    prepare(g + 2)
-                if not sums_on_tensor(g):
-                    add_sums(g)
+                if g + 4 < PASSES:
+                    prepare(g + 4)
+                if g + 5 < PASSES and helped_by_pool(g + 5):
+                    regroup_w_on_pool(g + 5)
+                if g + 2 < PASSES and not sums_on_tensor(g + 2):
+                    add_pairs(g + 2)
+                if g + 1 < PASSES and not sums_on_tensor(g + 1):
+                    add_sums(g + 1)
                 if g + 1 < PASSES and regroup_on_vector(g + 1):
                     regroup_w(g + 1)
-                if g >= 1:
-                    quantise_ax(g - 1)
-                    multiply(g - 1)
-                if g + 1 < PASSES:
-                    if not sums_on_tensor(g + 1):
-                        add_pairs(g + 1)
-                    quantise_w(g + 1)
-            quantise_ax(PASSES - 1)
-            multiply(PASSES - 1)
+                if g < PASSES - 1:
+                    quantise(g, 0, NODES + F_OUT)
+                else:
+                    quantise(g, NODES, NODES + F_OUT)
+                    quantise(g, 0, NODES)
+                multiply(g)
 
             for r in range(NODE_TILES):
                 result = results.tile([P, F_OUT], F32, name="result")

@@ -21,28 +21,28 @@ F_IN = 16384
 F_OUT = 512
 PASSES = F_IN // K_PASS
 NODE_TILES = NODES // P
-POOL_COLUMNS = 256
+POOL_COLUMNS = 128
+POOL_ROWS = 2
 LOADS_AHEAD = 6
 LINE = GRID * PACK
 TOP_TO_BOTTOM = (GRID - 1) * LINE + PACK
 SUMS = GRID + 1
 PAIR_PITCH = (SUMS + 1) * PACK
+VALUE_TILES = 7
 PAIR_TILES = 4
 MID_FIRST = 64
 
 FLOPS = 2 * NODES * F_IN * F_OUT + 3 * NODES * F_IN + NODES * F_OUT
 
 
-def sums_on_tensor(g):
-    return (3 * g + 3) % 8 < 3
-
-
-def helped_by_pool(g):
-    return g >= 5 and not sums_on_tensor(g - 3)
+def tensor_batches(g):
+    if (3 * g + 3) % 8 < 3:
+        return BATCH
+    return 1 if g == PASSES - 2 else 0
 
 
 def regroup_on_vector(g):
-    return g == 0
+    return g < 3
 
 
 def tile_graphconvlayer_k_kernel(tc, X, W_gcn, b, H, Wd, out):
@@ -55,9 +55,9 @@ def tile_graphconvlayer_k_kernel(tc, X, W_gcn, b, H, Wd, out):
     with ExitStack() as ctx:
         const = ctx.enter_context(tc.tile_pool(name="const", bufs=1))
         loads = ctx.enter_context(tc.tile_pool(name="loads", bufs=LOADS_AHEAD + 2))
-        regrouped = ctx.enter_context(tc.tile_pool(name="regrouped", bufs=6))
+        regrouped = ctx.enter_context(tc.tile_pool(name="regrouped", bufs=VALUE_TILES))
         turned = ctx.enter_context(tc.tile_pool(name="turned", bufs=3))
-        quant = ctx.enter_context(tc.tile_pool(name="quant", bufs=3))
+        quant = ctx.enter_context(tc.tile_pool(name="quant", bufs=5))
         results = ctx.enter_context(tc.tile_pool(name="results", bufs=NODE_TILES))
         acc_pool = ctx.enter_context(tc.psum_pool(name="acc", bufs=1))
         xt_pool = ctx.enter_context(tc.psum_pool(name="xt", bufs=4))
@@ -96,12 +96,14 @@ def tile_graphconvlayer_k_kernel(tc, X, W_gcn, b, H, Wd, out):
         acc = [acc_pool.tile([P, F_OUT], F32, name="acc%d" % r) for r in range(NODE_TILES)]
         bias = const.tile([P, F_OUT], BF16, name="bias")
 
+        on_vector = [g for g in range(PASSES) if tensor_batches(g) < BATCH]
         x_pass = {}
         x_middle = {}
         w_pass = {}
         x_turned = {}
         x_psum = {}
         grouped = {}
+        pooled = set()
         codes = {}
         scales = {}
 
@@ -115,13 +117,18 @@ def tile_graphconvlayer_k_kernel(tc, X, W_gcn, b, H, Wd, out):
         def load(g):
             features = slice(g * K_PASS, (g + 1) * K_PASS)
             x_sb = loads.tile([P, NODE_TILES, K_PASS], BF16, name="x_sb")
-            nc.sync.dma_start(out=x_sb[:], in_=x_rows[:, :, features])
+            if g == 0:
+                for bb in range(BATCH):
+                    tiles = slice(2 * bb, 2 * bb + 2)
+                    nc.sync.dma_start(out=x_sb[:, tiles], in_=x_rows[:, tiles, features])
+            else:
+                nc.sync.dma_start(out=x_sb[:], in_=x_rows[:, :, features])
             x_pass[g] = x_sb
-            if sums_on_tensor(g):
+            if tensor_batches(g) > 0:
                 x_mid = loads.tile([P, BATCH, K_PASS], BF16, name="x_mid")
                 nc.sync.dma_start(
-                    out=x_mid[:],
-                    in_=X[:, MID_FIRST : MID_FIRST + P, features].rearrange("b p f -> p b f"),
+                    out=x_mid[:, 0 : tensor_batches(g)],
+                    in_=X[0 : tensor_batches(g), MID_FIRST : MID_FIRST + P, features].rearrange("b p f -> p b f"),
                 )
                 x_middle[g] = x_mid
             w_sb = loads.tile([P, PACK, F_OUT], BF16, name="w_sb")
@@ -137,7 +144,7 @@ def tile_graphconvlayer_k_kernel(tc, X, W_gcn, b, H, Wd, out):
         def transpose_x(g):
             words = x_pass[g][:].bitcast(F32)
             xt_sb = turned.tile([P, BATCH, 2 * TOP_TO_BOTTOM], BF16, name="xt_sb", align_bytes=64)
-            for bb in range(BATCH):
+            for bb in range(tensor_batches(g), BATCH):
                 xt = xt_pool.tile([P, GRID * GRID, 2], F32, name="xt")
                 for u in range(2):
                     for half in range(2):
@@ -154,7 +161,7 @@ def tile_graphconvlayer_k_kernel(tc, X, W_gcn, b, H, Wd, out):
         def sum_on_tensor(g):
             ax = values(g)[:, 0:NODES].rearrange("p (b n) t -> p b n t", b=BATCH)
             edge = P - GRID
-            for bb in range(BATCH):
+            for bb in range(tensor_batches(g)):
                 bank = xt_pool.tile([P, PACK, GRID * GRID], BF16, name="xt")
                 for t in range(PACK):
                     x_up = x_pass[g][:, 2 * bb, t:K_PASS:PACK]
@@ -169,7 +176,7 @@ def tile_graphconvlayer_k_kernel(tc, X, W_gcn, b, H, Wd, out):
                 nc.scalar.copy(out=ax[:, bb], in_=bank[:].rearrange("p t n -> p n t"))
 
         def regroup_w(g):
-            first = POOL_COLUMNS if helped_by_pool(g) else 0
+            first = POOL_COLUMNS if g in pooled else 0
             rows = w_pass[g][:, :, first:]
             copy = nc.vector.tensor_copy if regroup_on_vector(g) else nc.scalar.copy
             copy(
@@ -178,6 +185,7 @@ def tile_graphconvlayer_k_kernel(tc, X, W_gcn, b, H, Wd, out):
             )
 
         def regroup_w_on_pool(g):
+            pooled.add(g)
             nc.gpsimd.tensor_scalar(
                 out=values(g)[:, NODES : NODES + POOL_COLUMNS],
                 in0=w_pass[g][:, :, 0:POOL_COLUMNS].rearrange("p t o -> p o t"),
@@ -188,9 +196,10 @@ def tile_graphconvlayer_k_kernel(tc, X, W_gcn, b, H, Wd, out):
             )
 
         def copy_single_terms(g):
-            runs = x_turned[g][:].rearrange("p b (e s) -> p b e s", e=2)
-            src = grid(x_turned[g])
-            pair = pair_tiles[g % PAIR_TILES]
+            batches = slice(tensor_batches(g), BATCH)
+            runs = x_turned[g][:].rearrange("p b (e s) -> p b e s", e=2)[:, batches]
+            src = grid(x_turned[g])[:, batches]
+            pair = pair_tiles[on_vector.index(g) % PAIR_TILES][:, batches]
             nc.scalar.copy(
                 out=pair[:, :, 0:SUMS:GRID, PACK:LINE], in_=runs[:, :, :, 0 : LINE - PACK]
             )
@@ -201,20 +210,22 @@ def tile_graphconvlayer_k_kernel(tc, X, W_gcn, b, H, Wd, out):
             )
 
         def add_pairs(g):
-            for bb in range(BATCH):
+            for bb in range(tensor_batches(g), BATCH):
                 nc.vector.tensor_tensor(
-                    out=pair_tiles[g % PAIR_TILES][:, bb, 1:GRID, PACK:LINE],
+                    out=pair_tiles[on_vector.index(g) % PAIR_TILES][:, bb, 1:GRID, PACK:LINE],
                     in0=x_psum[g, bb][:, 0 : GRID - 1, PACK:LINE],
                     in1=grid(x_turned[g])[:, bb, 1:GRID, 0 : LINE - PACK],
                     op=ADD,
                 )
 
-        def add_sums(g):
-            pair = pair_tiles[g % PAIR_TILES]
-            nc.vector.tensor_tensor(
-                out=values(g)[:, 0:NODES].rearrange("p (b i j) t -> p b i (j t)", b=BATCH, i=GRID),
-                in0=pair[:, :, 0:GRID, 0:LINE],
-                in1=pair[:, :, 1:SUMS, PACK : PACK + LINE],
+        def add_sums(engine, g, first, last):
+            batches = slice(tensor_batches(g), BATCH)
+            pair = pair_tiles[on_vector.index(g) % PAIR_TILES][:, batches]
+            ax = values(g)[:, 0:NODES].rearrange("p (b i j) t -> p b i (j t)", b=BATCH, i=GRID)
+            engine.tensor_tensor(
+                out=ax[:, batches, first:last],
+                in0=pair[:, :, first:last, 0:LINE],
+                in1=pair[:, :, first + 1 : last + 1, PACK : PACK + LINE],
                 op=ADD,
             )
 
@@ -244,46 +255,61 @@ def tile_graphconvlayer_k_kernel(tc, X, W_gcn, b, H, Wd, out):
         def prepare(g):
             if g + LOADS_AHEAD < PASSES:
                 load(g + LOADS_AHEAD)
-            if sums_on_tensor(g):
-                if not regroup_on_vector(g):
-                    regroup_w(g)
-                sum_on_tensor(g)
-            else:
+            if tensor_batches(g) < BATCH:
                 transpose_x(g)
-                if not regroup_on_vector(g):
-                    regroup_w(g)
+            if not regroup_on_vector(g):
+                regroup_w(g)
+            if tensor_batches(g) > 0:
+                sum_on_tensor(g)
+            if tensor_batches(g) < BATCH:
                 copy_single_terms(g)
 
         with tc.manual_schedule():
             for g in range(LOADS_AHEAD):
                 load(g)
             prepare(0)
-            if regroup_on_vector(0):
-                regroup_w(0)
+            regroup_w(0)
             add_pairs(0)
             prepare(1)
+            regroup_w(1)
             nc.sync.dma_start(out=bias[:], in_=b.partition_broadcast(P))
-            prepare(2)
-            add_pairs(1)
-            add_sums(0)
-            prepare(3)
-            for g in range(PASSES):
-                if g + 4 < PASSES:
-                    prepare(g + 4)
-                if g + 5 < PASSES and helped_by_pool(g + 5):
-                    regroup_w_on_pool(g + 5)
-                if g + 2 < PASSES and not sums_on_tensor(g + 2):
-                    add_pairs(g + 2)
-                if g + 1 < PASSES and not sums_on_tensor(g + 1):
-                    add_sums(g + 1)
-                if g + 1 < PASSES and regroup_on_vector(g + 1):
-                    regroup_w(g + 1)
-                if g < PASSES - 1:
-                    quantise(g, 0, NODES + F_OUT)
-                else:
-                    quantise(g, NODES, NODES + F_OUT)
-                    quantise(g, 0, NODES)
-                multiply(g)
+            prepared = 2
+            quantised = 0
+            multiplied = 0
+            for k, g in enumerate(on_vector):
+                following = on_vector[k + 1] if k + 1 < len(on_vector) else PASSES
+                freed = quantised - 1 + VALUE_TILES
+                helped = following < PASSES and VALUE_TILES <= freed < PASSES
+                for p in range(prepared, min(following + 3, PASSES)):
+                    if helped and p == freed:
+                        regroup_w_on_pool(freed)
+                    prepare(p)
+                    prepared = p + 1
+                if helped and prepared == freed:
+                    regroup_w_on_pool(freed)
+                pool_rows = POOL_ROWS if freed in pooled else 0
+                if pool_rows > 0:
+                    add_sums(nc.gpsimd, g, 0, pool_rows)
+                if following < PASSES:
+                    add_pairs(following)
+                add_sums(nc.vector, g, pool_rows, GRID)
+                if g == 0:
+                    regroup_w(2)
+                for p in range(multiplied, quantised):
+                    multiply(p)
+                multiplied = quantised
+                for p in range(quantised, g):
+                    quantise(p, 0, NODES + F_OUT)
+                quantised = g
+
+            for p in range(quantised, PASSES - 1):
+                quantise(p, 0, NODES + F_OUT)
+            for p in range(multiplied, PASSES - 1):
+                multiply(p)
+            quantise(PASSES - 1, NODES, NODES + F_OUT)
+            for r in range(NODE_TILES):
+                quantise(PASSES - 1, r * P, (r + 1) * P)
+            multiply(PASSES - 1)
 
             for r in range(NODE_TILES):
                 result = results.tile([P, F_OUT], F32, name="result")

@@ -9,7 +9,6 @@ U32 = mybir.dt.uint32
 U8 = mybir.dt.uint8
 FP8X4 = mybir.dt.float8_e4m3fn_x4
 ADD = mybir.AluOpType.add
-MULT = mybir.AluOpType.mult
 
 P = 128
 PACK = 4
@@ -21,24 +20,24 @@ F_IN = 16384
 F_OUT = 512
 PASSES = F_IN // K_PASS
 NODE_TILES = NODES // P
-POOL_COLUMNS = 128
-POOL_ROWS = 2
+POOL_ROWS = 8
 LOADS_AHEAD = 6
 LINE = GRID * PACK
-TOP_TO_BOTTOM = (GRID - 1) * LINE + PACK
+EVEN_ROWS = GRID // 2 + 1
+EVEN_PITCH = (GRID + 2) * PACK
 SUMS = GRID + 1
 PAIR_PITCH = (SUMS + 1) * PACK
 VALUE_TILES = 7
-PAIR_TILES = 4
+SUM_TILES = 4
 MID_FIRST = 64
 
 FLOPS = 2 * NODES * F_IN * F_OUT + 3 * NODES * F_IN + NODES * F_OUT
 
 
 def tensor_batches(g):
-    if (3 * g + 3) % 8 < 3:
+    if g % 3 == 2 or g >= PASSES - 3:
         return BATCH
-    return 1 if g == PASSES - 2 else 0
+    return 1 if g == PASSES - 4 else 0
 
 
 def regroup_on_vector(g):
@@ -56,7 +55,6 @@ def tile_graphconvlayer_k_kernel(tc, X, W_gcn, b, H, Wd, out):
         const = ctx.enter_context(tc.tile_pool(name="const", bufs=1))
         loads = ctx.enter_context(tc.tile_pool(name="loads", bufs=LOADS_AHEAD + 2))
         regrouped = ctx.enter_context(tc.tile_pool(name="regrouped", bufs=VALUE_TILES))
-        turned = ctx.enter_context(tc.tile_pool(name="turned", bufs=3))
         quant = ctx.enter_context(tc.tile_pool(name="quant", bufs=5))
         results = ctx.enter_context(tc.tile_pool(name="results", bufs=NODE_TILES))
         acc_pool = ctx.enter_context(tc.psum_pool(name="acc", bufs=1))
@@ -67,9 +65,15 @@ def tile_graphconvlayer_k_kernel(tc, X, W_gcn, b, H, Wd, out):
 
         pair_tiles = [
             const.tile([P, BATCH, SUMS, PAIR_PITCH], F32, name="pair%d" % s)
-            for s in range(PAIR_TILES)
+            for s in range(SUM_TILES)
         ]
-        for s in range(PAIR_TILES):
+        even_tiles = [
+            const.tile([P, BATCH, EVEN_ROWS, EVEN_PITCH], BF16, name="even%d" % s)
+            for s in range(SUM_TILES)
+        ]
+        for s in range(SUM_TILES):
+            nc.gpsimd.memset(even_tiles[s][:, :, 0 : GRID // 2, LINE:], 0.0)
+            nc.gpsimd.memset(even_tiles[s][:, :, GRID // 2, :], 0.0)
             nc.gpsimd.memset(pair_tiles[s][:, :, 0, 0:PACK], 0.0)
             nc.gpsimd.memset(pair_tiles[s][:, :, GRID, LINE : LINE + PACK], 0.0)
 
@@ -100,10 +104,8 @@ def tile_graphconvlayer_k_kernel(tc, X, W_gcn, b, H, Wd, out):
         x_pass = {}
         x_middle = {}
         w_pass = {}
-        x_turned = {}
         x_psum = {}
         grouped = {}
-        pooled = set()
         codes = {}
         scales = {}
 
@@ -138,12 +140,11 @@ def tile_graphconvlayer_k_kernel(tc, X, W_gcn, b, H, Wd, out):
             )
             w_pass[g] = w_sb
 
-        def grid(xt_sb):
-            return xt_sb[:, :, 0 : GRID * LINE].rearrange("p b (i c) -> p b i c", c=LINE)
+        def sum_tile(tiles, g):
+            return tiles[on_vector.index(g) % SUM_TILES]
 
         def transpose_x(g):
             words = x_pass[g][:].bitcast(F32)
-            xt_sb = turned.tile([P, BATCH, 2 * TOP_TO_BOTTOM], BF16, name="xt_sb", align_bytes=64)
             for bb in range(tensor_batches(g), BATCH):
                 xt = xt_pool.tile([P, GRID * GRID, 2], F32, name="xt")
                 for u in range(2):
@@ -154,9 +155,11 @@ def tile_graphconvlayer_k_kernel(tc, X, W_gcn, b, H, Wd, out):
                             ident[:],
                         )
                 words_out = xt[:].rearrange("p n u -> p (n u)")
-                nc.scalar.copy(out=xt_sb[:, bb, 0 : GRID * LINE].bitcast(F32), in_=words_out)
+                nc.scalar.copy(
+                    out=sum_tile(even_tiles, g)[:, bb, 0 : GRID // 2, 0:LINE].bitcast(F32),
+                    in_=words_out.rearrange("p (i w) -> p i w", i=GRID)[:, 0:GRID:2],
+                )
                 x_psum[g, bb] = words_out.bitcast(BF16).rearrange("p (i c) -> p i c", c=LINE)
-            x_turned[g] = xt_sb
 
         def sum_on_tensor(g):
             ax = values(g)[:, 0:NODES].rearrange("p (b n) t -> p b n t", b=BATCH)
@@ -176,51 +179,47 @@ def tile_graphconvlayer_k_kernel(tc, X, W_gcn, b, H, Wd, out):
                 nc.scalar.copy(out=ax[:, bb], in_=bank[:].rearrange("p t n -> p n t"))
 
         def regroup_w(g):
-            first = POOL_COLUMNS if g in pooled else 0
-            rows = w_pass[g][:, :, first:]
             copy = nc.vector.tensor_copy if regroup_on_vector(g) else nc.scalar.copy
             copy(
-                out=values(g)[:, NODES + first :].rearrange("p (c i) t -> p c t i", i=4),
-                in_=rows.rearrange("p t (c i) -> p c t i", i=4),
-            )
-
-        def regroup_w_on_pool(g):
-            pooled.add(g)
-            nc.gpsimd.tensor_scalar(
-                out=values(g)[:, NODES : NODES + POOL_COLUMNS],
-                in0=w_pass[g][:, :, 0:POOL_COLUMNS].rearrange("p t o -> p o t"),
-                scalar1=1.0,
-                scalar2=0.0,
-                op0=MULT,
-                op1=ADD,
+                out=values(g)[:, NODES:].rearrange("p (c i) t -> p c t i", i=4),
+                in_=w_pass[g][:].rearrange("p t (c i) -> p c t i", i=4),
             )
 
         def copy_single_terms(g):
             batches = slice(tensor_batches(g), BATCH)
-            runs = x_turned[g][:].rearrange("p b (e s) -> p b e s", e=2)[:, batches]
-            src = grid(x_turned[g])[:, batches]
-            pair = pair_tiles[on_vector.index(g) % PAIR_TILES][:, batches]
+            even = sum_tile(even_tiles, g)[:, batches]
+            pair = sum_tile(pair_tiles, g)[:, batches]
+            nc.scalar.copy(out=pair[:, :, 0, PACK:LINE], in_=even[:, :, 0, 0 : LINE - PACK])
+            nc.scalar.copy(out=pair[:, :, 1:GRID:2, 0:PACK], in_=even[:, :, 0 : GRID // 2, 0:PACK])
             nc.scalar.copy(
-                out=pair[:, :, 0:SUMS:GRID, PACK:LINE], in_=runs[:, :, :, 0 : LINE - PACK]
-            )
-            nc.scalar.copy(out=pair[:, :, 1:GRID, 0:PACK], in_=src[:, :, 0 : GRID - 1, 0:PACK])
-            nc.scalar.copy(
-                out=pair[:, :, 1:GRID, LINE : LINE + PACK],
-                in_=src[:, :, 1:GRID, LINE - PACK : LINE],
+                out=pair[:, :, 2:GRID:2, LINE : LINE + PACK],
+                in_=even[:, :, 1 : GRID // 2, LINE - PACK : LINE],
             )
 
         def add_pairs(g):
             for bb in range(tensor_batches(g), BATCH):
+                odd = x_psum[g, bb][:, 1:GRID:2]
+                even = sum_tile(even_tiles, g)[:, bb]
+                pair = sum_tile(pair_tiles, g)[:, bb]
                 nc.vector.tensor_tensor(
-                    out=pair_tiles[on_vector.index(g) % PAIR_TILES][:, bb, 1:GRID, PACK:LINE],
-                    in0=x_psum[g, bb][:, 0 : GRID - 1, PACK:LINE],
-                    in1=grid(x_turned[g])[:, bb, 1:GRID, 0 : LINE - PACK],
+                    out=pair[:, 1:GRID:2, PACK : PACK + LINE],
+                    in0=odd,
+                    in1=even[:, 0 : GRID // 2, PACK : PACK + LINE],
+                    op=ADD,
+                )
+                left = even.rearrange("p m c -> p (m c)")[
+                    :, EVEN_PITCH - PACK : EVEN_ROWS * EVEN_PITCH - PACK
+                ]
+                nc.vector.tensor_tensor(
+                    out=pair[:, 2:SUMS:2, 0:LINE],
+                    in0=odd,
+                    in1=left.rearrange("p (m c) -> p m c", c=EVEN_PITCH)[:, :, 0:LINE],
                     op=ADD,
                 )
 
         def add_sums(engine, g, first, last):
             batches = slice(tensor_batches(g), BATCH)
-            pair = pair_tiles[on_vector.index(g) % PAIR_TILES][:, batches]
+            pair = sum_tile(pair_tiles, g)[:, batches]
             ax = values(g)[:, 0:NODES].rearrange("p (b i j) t -> p b i (j t)", b=BATCH, i=GRID)
             engine.tensor_tensor(
                 out=ax[:, batches, first:last],
@@ -278,18 +277,13 @@ def tile_graphconvlayer_k_kernel(tc, X, W_gcn, b, H, Wd, out):
             multiplied = 0
             for k, g in enumerate(on_vector):
                 following = on_vector[k + 1] if k + 1 < len(on_vector) else PASSES
-                freed = quantised - 1 + VALUE_TILES
-                helped = following < PASSES and VALUE_TILES <= freed < PASSES
+                pool_rows = POOL_ROWS if quantised > 0 and following < PASSES else 0
+                if pool_rows > 0:
+                    nc.gpsimd.memset(values(quantised - 1)[:, 0:GRID], 0.0)
+                    add_sums(nc.gpsimd, g, 0, pool_rows)
                 for p in range(prepared, min(following + 3, PASSES)):
-                    if helped and p == freed:
-                        regroup_w_on_pool(freed)
                     prepare(p)
                     prepared = p + 1
-                if helped and prepared == freed:
-                    regroup_w_on_pool(freed)
-                pool_rows = POOL_ROWS if freed in pooled else 0
-                if pool_rows > 0:
-                    add_sums(nc.gpsimd, g, 0, pool_rows)
                 if following < PASSES:
                     add_pairs(following)
                 add_sums(nc.vector, g, pool_rows, GRID)

@@ -63,6 +63,9 @@ def tile_graphconvlayer_k_kernel(tc, X, W_gcn, b, H, Wd, out):
         ident = const.tile([P, P], F32, name="ident")
         masks.make_identity(nc, ident[:])
 
+        def zero_corner(pair):
+            nc.gpsimd.memset(pair[:, :, GRID, LINE : LINE + PACK], 0.0)
+
         pair_tiles = [
             const.tile([P, BATCH, SUMS, PAIR_PITCH], F32, name="pair%d" % s)
             for s in range(SUM_TILES)
@@ -75,7 +78,7 @@ def tile_graphconvlayer_k_kernel(tc, X, W_gcn, b, H, Wd, out):
             nc.gpsimd.memset(even_tiles[s][:, :, 0 : GRID // 2, LINE:], 0.0)
             nc.gpsimd.memset(even_tiles[s][:, :, GRID // 2, :], 0.0)
             nc.gpsimd.memset(pair_tiles[s][:, :, 0, 0:PACK], 0.0)
-            nc.gpsimd.memset(pair_tiles[s][:, :, GRID, LINE : LINE + PACK], 0.0)
+            zero_corner(pair_tiles[s])
 
         wide = const.tile([P, P + 2 * GRID], BF16, name="wide")
         nc.vector.memset(wide[:], 0.0)
@@ -190,10 +193,11 @@ def tile_graphconvlayer_k_kernel(tc, X, W_gcn, b, H, Wd, out):
             even = sum_tile(even_tiles, g)[:, batches]
             pair = sum_tile(pair_tiles, g)[:, batches]
             nc.scalar.copy(out=pair[:, :, 0, PACK:LINE], in_=even[:, :, 0, 0 : LINE - PACK])
-            nc.scalar.copy(out=pair[:, :, 1:GRID:2, 0:PACK], in_=even[:, :, 0 : GRID // 2, 0:PACK])
+            ends = pair[:, :, 0:GRID].rearrange("p b (m r) c -> p b m (r c)", r=2)
+            ends = ends.rearrange("p b m (n t) -> p b m n t", t=PACK)
+            nodes = even[:, :, 0 : GRID // 2].rearrange("p b m (n t) -> p b m n t", t=PACK)
             nc.scalar.copy(
-                out=pair[:, :, 2:GRID:2, LINE : LINE + PACK],
-                in_=even[:, :, 1 : GRID // 2, LINE - PACK : LINE],
+                out=ends[:, :, :, GRID : SUMS + 2 : 2], in_=nodes[:, :, :, GRID - 1 :: 1 - GRID]
             )
 
         def add_pairs(g):
@@ -238,8 +242,8 @@ def tile_graphconvlayer_k_kernel(tc, X, W_gcn, b, H, Wd, out):
                 in_=values(g)[:, first:last].rearrange("p n t -> p (n t)"),
             )
 
-        def multiply(g):
-            for r in range(NODE_TILES):
+        def multiply(g, node_tiles=range(NODE_TILES)):
+            for r in node_tiles:
                 nodes = slice(r * P, (r + 1) * P)
                 nc.tensor.matmul_mx(
                     out=acc[r][:],
@@ -277,35 +281,39 @@ def tile_graphconvlayer_k_kernel(tc, X, W_gcn, b, H, Wd, out):
             multiplied = 0
             for k, g in enumerate(on_vector):
                 following = on_vector[k + 1] if k + 1 < len(on_vector) else PASSES
-                pool_rows = POOL_ROWS if quantised > 0 and following < PASSES else 0
+                pool_rows = POOL_ROWS if k > 0 and following < PASSES else 0
                 if pool_rows > 0:
-                    nc.gpsimd.memset(values(quantised - 1)[:, 0:GRID], 0.0)
+                    zero_corner(sum_tile(pair_tiles, on_vector[k - 1]))
                     add_sums(nc.gpsimd, g, 0, pool_rows)
                 for p in range(prepared, min(following + 3, PASSES)):
                     prepare(p)
                     prepared = p + 1
                 if following < PASSES:
                     add_pairs(following)
+                for p in range(quantised, g - 1):
+                    quantise(p, 0, NODES + F_OUT)
                 add_sums(nc.vector, g, pool_rows, GRID)
                 if g == 0:
                     regroup_w(2)
                 for p in range(multiplied, quantised):
                     multiply(p)
                 multiplied = quantised
-                for p in range(quantised, g):
-                    quantise(p, 0, NODES + F_OUT)
+                if g > 0:
+                    quantise(g - 1, 0, NODES + F_OUT)
                 quantised = g
 
             for p in range(quantised, PASSES - 1):
                 quantise(p, 0, NODES + F_OUT)
             for p in range(multiplied, PASSES - 1):
                 multiply(p)
-            quantise(PASSES - 1, NODES, NODES + F_OUT)
-            for r in range(NODE_TILES):
-                quantise(PASSES - 1, r * P, (r + 1) * P)
-            multiply(PASSES - 1)
-
-            for r in range(NODE_TILES):
-                result = results.tile([P, F_OUT], F32, name="result")
-                nc.vector.tensor_tensor(out=result[:], in0=acc[r][:], in1=bias[:], op=ADD)
-                nc.sync.dma_start(out=out_rows[r * P : (r + 1) * P, :], in_=result[:])
+            last = PASSES - 1
+            quantise(last, NODES, NODES + F_OUT)
+            for bb in range(BATCH):
+                node_tiles = range(2 * bb, 2 * bb + 2)
+                for r in node_tiles:
+                    quantise(last, r * P, (r + 1) * P)
+                multiply(last, node_tiles)
+                for r in node_tiles:
+                    result = results.tile([P, F_OUT], F32, name="result")
+                    nc.vector.tensor_tensor(out=result[:], in0=acc[r][:], in1=bias[:], op=ADD)
+                    nc.sync.dma_start(out=out_rows[r * P : (r + 1) * P, :], in_=result[:])

@@ -9,6 +9,7 @@ U32 = mybir.dt.uint32
 U8 = mybir.dt.uint8
 FP8X4 = mybir.dt.float8_e4m3fn_x4
 ADD = mybir.AluOpType.add
+MULT = mybir.AluOpType.mult
 
 P = 128
 PACK = 4
@@ -22,11 +23,8 @@ PASSES = F_IN // K_PASS
 NODE_TILES = NODES // P
 POOL_ROWS = 8
 LOADS_AHEAD = 6
-LINE = GRID * PACK
-EVEN_ROWS = GRID // 2 + 1
-EVEN_PITCH = (GRID + 2) * PACK
+HALF = GRID // 2
 SUMS = GRID + 1
-PAIR_PITCH = (SUMS + 1) * PACK
 VALUE_TILES = 7
 SUM_TILES = 4
 MID_FIRST = 64
@@ -40,15 +38,16 @@ def tensor_batches(g):
     return 1 if g == PASSES - 4 else 0
 
 
-def regroup_on_vector(g):
-    return g < 3
+def regroup_on_pool(g):
+    return g in (0, 2, PASSES - 1)
 
 
 def tile_graphconvlayer_k_kernel(tc, X, W_gcn, b, H, Wd, out):
     nc = tc.nc
     assert H == GRID and Wd == GRID
 
-    x_rows = X.rearrange("b n f -> (b n) f").rearrange("(r p) f -> p r f", p=P)
+    x_halves = X.rearrange("b (h p) f -> h p b f", p=P)
+    x_columns = X.rearrange("b (p e) f -> e p b f", p=P)
     out_rows = out.rearrange("b n o -> (b n) o")
 
     with ExitStack() as ctx:
@@ -64,21 +63,22 @@ def tile_graphconvlayer_k_kernel(tc, X, W_gcn, b, H, Wd, out):
         masks.make_identity(nc, ident[:])
 
         def zero_corner(pair):
-            nc.gpsimd.memset(pair[:, :, GRID, LINE : LINE + PACK], 0.0)
+            nc.gpsimd.memset(pair[:, 0, :, 0], 0.0)
 
         pair_tiles = [
-            const.tile([P, BATCH, SUMS, PAIR_PITCH], F32, name="pair%d" % s)
-            for s in range(SUM_TILES)
-        ]
-        even_tiles = [
-            const.tile([P, BATCH, EVEN_ROWS, EVEN_PITCH], BF16, name="even%d" % s)
+            const.tile([P, SUMS, BATCH, GRID + 2, PACK], F32, name="pair%d" % s)
             for s in range(SUM_TILES)
         ]
         for s in range(SUM_TILES):
-            nc.gpsimd.memset(even_tiles[s][:, :, 0 : GRID // 2, LINE:], 0.0)
-            nc.gpsimd.memset(even_tiles[s][:, :, GRID // 2, :], 0.0)
-            nc.gpsimd.memset(pair_tiles[s][:, :, 0, 0:PACK], 0.0)
             zero_corner(pair_tiles[s])
+            nc.gpsimd.memset(pair_tiles[s][:, GRID, :, GRID], 0.0)
+        even_tiles = [
+            const.tile([P, GRID + 2, BATCH, HALF + 2, PACK], BF16, name="even%d" % s)
+            for s in range(SUM_TILES)
+        ]
+        for s in range(SUM_TILES):
+            nc.gpsimd.memset(even_tiles[s][:, 0 : GRID + 2 : GRID + 1], 0.0)
+            nc.gpsimd.memset(even_tiles[s][:, 1 : GRID + 1, :, HALF:], 0.0)
 
         wide = const.tile([P, P + 2 * GRID], BF16, name="wide")
         nc.vector.memset(wide[:], 0.0)
@@ -107,7 +107,7 @@ def tile_graphconvlayer_k_kernel(tc, X, W_gcn, b, H, Wd, out):
         x_pass = {}
         x_middle = {}
         w_pass = {}
-        x_psum = {}
+        x_odd = {}
         grouped = {}
         codes = {}
         scales = {}
@@ -122,12 +122,14 @@ def tile_graphconvlayer_k_kernel(tc, X, W_gcn, b, H, Wd, out):
         def load(g):
             features = slice(g * K_PASS, (g + 1) * K_PASS)
             x_sb = loads.tile([P, NODE_TILES, K_PASS], BF16, name="x_sb")
-            if g == 0:
-                for bb in range(BATCH):
-                    tiles = slice(2 * bb, 2 * bb + 2)
-                    nc.sync.dma_start(out=x_sb[:, tiles], in_=x_rows[:, tiles, features])
-            else:
-                nc.sync.dma_start(out=x_sb[:], in_=x_rows[:, :, features])
+            count = tensor_batches(g)
+            for s in range(2):
+                for view, first, end in ((x_halves, 0, count), (x_columns, count, BATCH)):
+                    if first < end:
+                        nc.sync.dma_start(
+                            out=x_sb[:, 2 * s + first : 2 * s + end],
+                            in_=view[s][:, first:end, features],
+                        )
             x_pass[g] = x_sb
             if tensor_batches(g) > 0:
                 x_mid = loads.tile([P, BATCH, K_PASS], BF16, name="x_mid")
@@ -148,21 +150,29 @@ def tile_graphconvlayer_k_kernel(tc, X, W_gcn, b, H, Wd, out):
 
         def transpose_x(g):
             words = x_pass[g][:].bitcast(F32)
-            for bb in range(tensor_batches(g), BATCH):
-                xt = xt_pool.tile([P, GRID * GRID, 2], F32, name="xt")
-                for u in range(2):
-                    for half in range(2):
+            batches = slice(tensor_batches(g), BATCH)
+            for parity in range(2):
+                xt = xt_pool.tile([P, BATCH, P, 2], F32, name="xt")
+                for bb in range(tensor_batches(g), BATCH):
+                    for u in range(2):
                         nc.tensor.transpose(
-                            xt[:, half * P : (half + 1) * P, u],
-                            words[:, 2 * bb + half, u : 2 * P : 2],
-                            ident[:],
+                            xt[:, bb, :, u], words[:, 2 * parity + bb, u : 2 * P : 2], ident[:]
                         )
-                words_out = xt[:].rearrange("p n u -> p (n u)")
-                nc.scalar.copy(
-                    out=sum_tile(even_tiles, g)[:, bb, 0 : GRID // 2, 0:LINE].bitcast(F32),
-                    in_=words_out.rearrange("p (i w) -> p i w", i=GRID)[:, 0:GRID:2],
-                )
-                x_psum[g, bb] = words_out.bitcast(BF16).rearrange("p (i c) -> p i c", c=LINE)
+                nodes = xt[:].rearrange("p b (i m) u -> p i b (m u)", i=GRID)[:, :, batches]
+                if parity == 0:
+                    even = sum_tile(even_tiles, g)[:, 1 : GRID + 1, batches, 0:HALF]
+                    nc.scalar.copy(
+                        out=even.rearrange("p i b m t -> p i b (m t)").bitcast(F32), in_=nodes
+                    )
+                else:
+                    x_odd[g] = (
+                        xt[:]
+                        .rearrange("p b n u -> p (b n u)")
+                        .bitcast(BF16)
+                        .rearrange("p (b i m t) -> p i b m t", b=BATCH, i=GRID, t=PACK)[
+                            :, :, batches
+                        ]
+                    )
 
         def sum_on_tensor(g):
             ax = values(g)[:, 0:NODES].rearrange("p (b n) t -> p b n t", b=BATCH)
@@ -170,9 +180,9 @@ def tile_graphconvlayer_k_kernel(tc, X, W_gcn, b, H, Wd, out):
             for bb in range(tensor_batches(g)):
                 bank = xt_pool.tile([P, PACK, GRID * GRID], BF16, name="xt")
                 for t in range(PACK):
-                    x_up = x_pass[g][:, 2 * bb, t:K_PASS:PACK]
+                    x_up = x_pass[g][:, bb, t:K_PASS:PACK]
                     x_mid = x_middle[g][:, bb, t:K_PASS:PACK]
-                    x_low = x_pass[g][:, 2 * bb + 1, t:K_PASS:PACK]
+                    x_low = x_pass[g][:, 2 + bb, t:K_PASS:PACK]
                     for dst, lhsT, columns in (
                         (bank[:, t, 0:edge], x_up, adjacency[:, 0:edge]),
                         (bank[:, t, edge : P + GRID], x_mid, adjacency[:, 3 * GRID : 5 * GRID]),
@@ -182,53 +192,54 @@ def tile_graphconvlayer_k_kernel(tc, X, W_gcn, b, H, Wd, out):
                 nc.scalar.copy(out=ax[:, bb], in_=bank[:].rearrange("p t n -> p n t"))
 
         def regroup_w(g):
-            copy = nc.vector.tensor_copy if regroup_on_vector(g) else nc.scalar.copy
-            copy(
+            if regroup_on_pool(g):
+                nc.gpsimd.tensor_scalar(
+                    out=values(g)[:, NODES:],
+                    in0=w_pass[g][:].rearrange("p t o -> p o t"),
+                    scalar1=1.0,
+                    scalar2=0.0,
+                    op0=MULT,
+                    op1=ADD,
+                )
+                return
+            nc.scalar.copy(
                 out=values(g)[:, NODES:].rearrange("p (c i) t -> p c t i", i=4),
                 in_=w_pass[g][:].rearrange("p t (c i) -> p c t i", i=4),
             )
 
         def copy_single_terms(g):
             batches = slice(tensor_batches(g), BATCH)
-            even = sum_tile(even_tiles, g)[:, batches]
-            pair = sum_tile(pair_tiles, g)[:, batches]
-            nc.scalar.copy(out=pair[:, :, 0, PACK:LINE], in_=even[:, :, 0, 0 : LINE - PACK])
-            ends = pair[:, :, 0:GRID].rearrange("p b (m r) c -> p b m (r c)", r=2)
-            ends = ends.rearrange("p b m (n t) -> p b m n t", t=PACK)
-            nodes = even[:, :, 0 : GRID // 2].rearrange("p b m (n t) -> p b m n t", t=PACK)
-            nc.scalar.copy(
-                out=ends[:, :, :, GRID : SUMS + 2 : 2], in_=nodes[:, :, :, GRID - 1 :: 1 - GRID]
-            )
+            even = sum_tile(even_tiles, g)
+            pair = sum_tile(pair_tiles, g)
+            nc.scalar.copy(out=pair[:, 0, batches, 1:GRID:2], in_=even[:, 1, batches, 0:HALF])
+            nc.scalar.copy(out=pair[:, GRID, batches, 2:GRID:2], in_=even[:, GRID, batches, 1:HALF])
+            nc.scalar.copy(out=pair[:, 1:GRID, batches, 0], in_=even[:, 1:GRID, batches, 0])
 
         def add_pairs(g):
-            for bb in range(tensor_batches(g), BATCH):
-                odd = x_psum[g, bb][:, 1:GRID:2]
-                even = sum_tile(even_tiles, g)[:, bb]
-                pair = sum_tile(pair_tiles, g)[:, bb]
-                nc.vector.tensor_tensor(
-                    out=pair[:, 1:GRID:2, PACK : PACK + LINE],
-                    in0=odd,
-                    in1=even[:, 0 : GRID // 2, PACK : PACK + LINE],
-                    op=ADD,
-                )
-                left = even.rearrange("p m c -> p (m c)")[
-                    :, EVEN_PITCH - PACK : EVEN_ROWS * EVEN_PITCH - PACK
-                ]
-                nc.vector.tensor_tensor(
-                    out=pair[:, 2:SUMS:2, 0:LINE],
-                    in0=odd,
-                    in1=left.rearrange("p (m c) -> p m c", c=EVEN_PITCH)[:, :, 0:LINE],
-                    op=ADD,
-                )
+            batches = slice(tensor_batches(g), BATCH)
+            even = sum_tile(even_tiles, g)
+            pair = sum_tile(pair_tiles, g)
+            nc.vector.tensor_tensor(
+                out=pair[:, 0:GRID, batches, 2:SUMS:2],
+                in0=x_odd[g],
+                in1=even[:, 0:GRID, batches, 1 : HALF + 1],
+                op=ADD,
+            )
+            nc.vector.tensor_tensor(
+                out=pair[:, 1:SUMS, batches, 1:GRID:2],
+                in0=x_odd[g],
+                in1=even[:, 2 : GRID + 2, batches, 0:HALF],
+                op=ADD,
+            )
 
         def add_sums(engine, g, first, last):
             batches = slice(tensor_batches(g), BATCH)
-            pair = sum_tile(pair_tiles, g)[:, batches]
-            ax = values(g)[:, 0:NODES].rearrange("p (b i j) t -> p b i (j t)", b=BATCH, i=GRID)
+            pair = sum_tile(pair_tiles, g)
+            ax = values(g)[:, 0:NODES].rearrange("p (b i j) t -> p i b j t", b=BATCH, i=GRID)
             engine.tensor_tensor(
-                out=ax[:, batches, first:last],
-                in0=pair[:, :, first:last, 0:LINE],
-                in1=pair[:, :, first + 1 : last + 1, PACK : PACK + LINE],
+                out=ax[:, first:last, batches],
+                in0=pair[:, first:last, batches, 0:GRID],
+                in1=pair[:, first + 1 : last + 1, batches, 1:SUMS],
                 op=ADD,
             )
 
@@ -260,8 +271,7 @@ def tile_graphconvlayer_k_kernel(tc, X, W_gcn, b, H, Wd, out):
                 load(g + LOADS_AHEAD)
             if tensor_batches(g) < BATCH:
                 transpose_x(g)
-            if not regroup_on_vector(g):
-                regroup_w(g)
+            regroup_w(g)
             if tensor_batches(g) > 0:
                 sum_on_tensor(g)
             if tensor_batches(g) < BATCH:
@@ -271,30 +281,31 @@ def tile_graphconvlayer_k_kernel(tc, X, W_gcn, b, H, Wd, out):
             for g in range(LOADS_AHEAD):
                 load(g)
             prepare(0)
-            regroup_w(0)
             add_pairs(0)
             prepare(1)
-            regroup_w(1)
             nc.sync.dma_start(out=bias[:], in_=b.partition_broadcast(P))
             prepared = 2
             quantised = 0
             multiplied = 0
             for k, g in enumerate(on_vector):
                 following = on_vector[k + 1] if k + 1 < len(on_vector) else PASSES
-                pool_rows = POOL_ROWS if k > 0 and following < PASSES else 0
+                beside = BATCH - tensor_batches(following) if following < PASSES else 0
+                pool_rows = POOL_ROWS * beside // BATCH
                 if pool_rows > 0:
-                    zero_corner(sum_tile(pair_tiles, on_vector[k - 1]))
-                    add_sums(nc.gpsimd, g, 0, pool_rows)
+                    if k > 0:
+                        zero_corner(sum_tile(pair_tiles, on_vector[k - 1]))
+                    add_sums(nc.gpsimd, g, GRID - pool_rows, GRID)
                 for p in range(prepared, min(following + 3, PASSES)):
+                    if p > prepared and multiplied < quantised:
+                        multiply(multiplied)
+                        multiplied += 1
                     prepare(p)
-                    prepared = p + 1
+                prepared = max(prepared, min(following + 3, PASSES))
                 if following < PASSES:
                     add_pairs(following)
                 for p in range(quantised, g - 1):
                     quantise(p, 0, NODES + F_OUT)
-                add_sums(nc.vector, g, pool_rows, GRID)
-                if g == 0:
-                    regroup_w(2)
+                add_sums(nc.vector, g, 0, GRID - pool_rows)
                 for p in range(multiplied, quantised):
                     multiply(p)
                 multiplied = quantised

@@ -39,7 +39,11 @@ def tensor_batches(g):
 
 
 def regroup_on_pool(g):
-    return g in (0, 2, PASSES - 1)
+    return g in (0, 3)
+
+
+def regroup_on_vector(g):
+    return g == PASSES // 2
 
 
 def tile_graphconvlayer_k_kernel(tc, X, W_gcn, b, H, Wd, out):
@@ -189,7 +193,12 @@ def tile_graphconvlayer_k_kernel(tc, X, W_gcn, b, H, Wd, out):
                         (bank[:, t, P + GRID :], x_low, adjacency[:, GRID:P]),
                     ):
                         nc.tensor.matmul(out=dst, lhsT=lhsT, rhs=columns, start=True, stop=True)
-                nc.scalar.copy(out=ax[:, bb], in_=bank[:].rearrange("p t n -> p n t"))
+                step = P if g == PASSES - 1 else GRID * GRID
+                for n in range(0, GRID * GRID, step):
+                    nc.scalar.copy(
+                        out=ax[:, bb, n : n + step],
+                        in_=bank[:, :, n : n + step].rearrange("p t n -> p n t"),
+                    )
 
         def regroup_w(g):
             if regroup_on_pool(g):
@@ -202,7 +211,8 @@ def tile_graphconvlayer_k_kernel(tc, X, W_gcn, b, H, Wd, out):
                     op1=ADD,
                 )
                 return
-            nc.scalar.copy(
+            copy = nc.vector.tensor_copy if regroup_on_vector(g) else nc.scalar.copy
+            copy(
                 out=values(g)[:, NODES:].rearrange("p (c i) t -> p c t i", i=4),
                 in_=w_pass[g][:].rearrange("p t (c i) -> p c t i", i=4),
             )
@@ -271,7 +281,8 @@ def tile_graphconvlayer_k_kernel(tc, X, W_gcn, b, H, Wd, out):
                 load(g + LOADS_AHEAD)
             if tensor_batches(g) < BATCH:
                 transpose_x(g)
-            regroup_w(g)
+            if not regroup_on_vector(g):
+                regroup_w(g)
             if tensor_batches(g) > 0:
                 sum_on_tensor(g)
             if tensor_batches(g) < BATCH:
@@ -295,16 +306,20 @@ def tile_graphconvlayer_k_kernel(tc, X, W_gcn, b, H, Wd, out):
                     if k > 0:
                         zero_corner(sum_tile(pair_tiles, on_vector[k - 1]))
                     add_sums(nc.gpsimd, g, GRID - pool_rows, GRID)
-                for p in range(prepared, min(following + 3, PASSES)):
-                    if p > prepared and multiplied < quantised:
+                fresh = range(prepared, max(prepared, min(following + 3, PASSES)))
+                for p in fresh:
+                    if multiplied < quantised:
                         multiply(multiplied)
                         multiplied += 1
                     prepare(p)
-                prepared = max(prepared, min(following + 3, PASSES))
+                prepared = fresh.stop
                 if following < PASSES:
                     add_pairs(following)
                 for p in range(quantised, g - 1):
                     quantise(p, 0, NODES + F_OUT)
+                for p in fresh:
+                    if regroup_on_vector(p):
+                        regroup_w(p)
                 add_sums(nc.vector, g, 0, GRID - pool_rows)
                 for p in range(multiplied, quantised):
                     multiply(p)
@@ -317,14 +332,16 @@ def tile_graphconvlayer_k_kernel(tc, X, W_gcn, b, H, Wd, out):
                 quantise(p, 0, NODES + F_OUT)
             for p in range(multiplied, PASSES - 1):
                 multiply(p)
+            def store(r):
+                result = results.tile([P, F_OUT], F32, name="result")
+                nc.vector.tensor_tensor(out=result[:], in0=acc[r][:], in1=bias[:], op=ADD)
+                nc.sync.dma_start(out=out_rows[r * P : (r + 1) * P, :], in_=result[:])
+
             last = PASSES - 1
             quantise(last, NODES, NODES + F_OUT)
-            for bb in range(BATCH):
-                node_tiles = range(2 * bb, 2 * bb + 2)
-                for r in node_tiles:
-                    quantise(last, r * P, (r + 1) * P)
-                multiply(last, node_tiles)
-                for r in node_tiles:
-                    result = results.tile([P, F_OUT], F32, name="result")
-                    nc.vector.tensor_tensor(out=result[:], in0=acc[r][:], in1=bias[:], op=ADD)
-                    nc.sync.dma_start(out=out_rows[r * P : (r + 1) * P, :], in_=result[:])
+            for r in range(NODE_TILES):
+                quantise(last, r * P, (r + 1) * P)
+                multiply(last, range(r, r + 1))
+                if r > 0:
+                    store(r - 1)
+            store(NODE_TILES - 1)

@@ -39,11 +39,7 @@ def tensor_batches(g):
 
 
 def regroup_on_pool(g):
-    return g in (0, 3)
-
-
-def regroup_on_vector(g):
-    return g == PASSES // 2
+    return g in (0, 2)
 
 
 def tile_graphconvlayer_k_kernel(tc, X, W_gcn, b, H, Wd, out):
@@ -211,8 +207,7 @@ def tile_graphconvlayer_k_kernel(tc, X, W_gcn, b, H, Wd, out):
                     op1=ADD,
                 )
                 return
-            copy = nc.vector.tensor_copy if regroup_on_vector(g) else nc.scalar.copy
-            copy(
+            nc.scalar.copy(
                 out=values(g)[:, NODES:].rearrange("p (c i) t -> p c t i", i=4),
                 in_=w_pass[g][:].rearrange("p t (c i) -> p c t i", i=4),
             )
@@ -281,8 +276,7 @@ def tile_graphconvlayer_k_kernel(tc, X, W_gcn, b, H, Wd, out):
                 load(g + LOADS_AHEAD)
             if tensor_batches(g) < BATCH:
                 transpose_x(g)
-            if not regroup_on_vector(g):
-                regroup_w(g)
+            regroup_w(g)
             if tensor_batches(g) > 0:
                 sum_on_tensor(g)
             if tensor_batches(g) < BATCH:
@@ -317,9 +311,6 @@ def tile_graphconvlayer_k_kernel(tc, X, W_gcn, b, H, Wd, out):
                     add_pairs(following)
                 for p in range(quantised, g - 1):
                     quantise(p, 0, NODES + F_OUT)
-                for p in fresh:
-                    if regroup_on_vector(p):
-                        regroup_w(p)
                 add_sums(nc.vector, g, 0, GRID - pool_rows)
                 for p in range(multiplied, quantised):
                     multiply(p)
@@ -332,16 +323,12 @@ def tile_graphconvlayer_k_kernel(tc, X, W_gcn, b, H, Wd, out):
                 quantise(p, 0, NODES + F_OUT)
             for p in range(multiplied, PASSES - 1):
                 multiply(p)
-            def store(r):
-                result = results.tile([P, F_OUT], F32, name="result")
-                nc.vector.tensor_tensor(out=result[:], in0=acc[r][:], in1=bias[:], op=ADD)
-                nc.sync.dma_start(out=out_rows[r * P : (r + 1) * P, :], in_=result[:])
-
             last = PASSES - 1
             quantise(last, NODES, NODES + F_OUT)
             for r in range(NODE_TILES):
                 quantise(last, r * P, (r + 1) * P)
                 multiply(last, range(r, r + 1))
-                if r > 0:
-                    store(r - 1)
-            store(NODE_TILES - 1)
+            for r in range(NODE_TILES):
+                result = results.tile([P, F_OUT], F32, name="result")
+                nc.vector.tensor_tensor(out=result[:], in0=acc[r][:], in1=bias[:], op=ADD)
+                nc.sync.dma_start(out=out_rows[r * P : (r + 1) * P, :], in_=result[:])

from contextlib import ExitStack

import concourse.masks as masks
import concourse.mybir as mybir

BF16 = mybir.dt.bfloat16
F32 = mybir.dt.float32
U32 = mybir.dt.uint32
U8 = mybir.dt.uint8
FP8X4 = mybir.dt.float8_e4m3fn_x4
ADD = mybir.AluOpType.add
MULT = mybir.AluOpType.mult

P = 128
PACK = 4
K_PASS = P * PACK
BATCH = 2
GRID = 16
NODES = BATCH * GRID * GRID
F_IN = 16384
F_OUT = 512
PASSES = F_IN // K_PASS
NODE_TILES = NODES // P
POOL_ROWS = 8
LOADS_AHEAD = 6
HALF = GRID // 2
SUMS = GRID + 1
VALUE_TILES = 7
SUM_TILES = 4
MID_FIRST = 64

FLOPS = 2 * NODES * F_IN * F_OUT + 3 * NODES * F_IN + NODES * F_OUT


def tensor_batches(g):
    if g % 3 == 2 or g >= PASSES - 3:
        return BATCH
    return 1 if g == PASSES - 4 else 0


def regroup_on_pool(g):
    return g in (0, 2)


def tile_graphconvlayer_k_kernel(tc, X, W_gcn, b, H, Wd, out):
    nc = tc.nc
    assert H == GRID and Wd == GRID

    x_halves = X.rearrange("b (h p) f -> h p b f", p=P)
    x_columns = X.rearrange("b (p e) f -> e p b f", p=P)
    out_rows = out.rearrange("b n o -> (b n) o")

    with ExitStack() as ctx:
        const = ctx.enter_context(tc.tile_pool(name="const", bufs=1))
        loads = ctx.enter_context(tc.tile_pool(name="loads", bufs=LOADS_AHEAD + 2))
        regrouped = ctx.enter_context(tc.tile_pool(name="regrouped", bufs=VALUE_TILES))
        quant = ctx.enter_context(tc.tile_pool(name="quant", bufs=5))
        results = ctx.enter_context(tc.tile_pool(name="results", bufs=NODE_TILES))
        acc_pool = ctx.enter_context(tc.psum_pool(name="acc", bufs=1))
        xt_pool = ctx.enter_context(tc.psum_pool(name="xt", bufs=4))

        ident = const.tile([P, P], F32, name="ident")
        masks.make_identity(nc, ident[:])

        def zero_corner(pair):
            nc.gpsimd.memset(pair[:, 0, :, 0], 0.0)

        pair_tiles = [
            const.tile([P, SUMS, BATCH, GRID + 2, PACK], F32, name="pair%d" % s)
            for s in range(SUM_TILES)
        ]
        for s in range(SUM_TILES):
            zero_corner(pair_tiles[s])
            nc.gpsimd.memset(pair_tiles[s][:, GRID, :, GRID], 0.0)
        even_tiles = [
            const.tile([P, GRID + 2, BATCH, HALF + 2, PACK], BF16, name="even%d" % s)
            for s in range(SUM_TILES)
        ]
        for s in range(SUM_TILES):
            nc.gpsimd.memset(even_tiles[s][:, 0 : GRID + 2 : GRID + 1], 0.0)
            nc.gpsimd.memset(even_tiles[s][:, 1 : GRID + 1, :, HALF:], 0.0)

        wide = const.tile([P, P + 2 * GRID], BF16, name="wide")
        nc.vector.memset(wide[:], 0.0)
        nc.vector.tensor_copy(out=wide[:, GRID : GRID + P], in_=ident[:])
        adjacency = const.tile([P, P], BF16, name="adjacency")
        nc.vector.tensor_tensor(
            out=adjacency[:], in0=wide[:, 0:P], in1=wide[:, 2 * GRID : 2 * GRID + P], op=ADD
        )
        by_row = adjacency[:].rearrange("p (i j) -> p i j", j=GRID)
        from_left = wide[:, GRID - 1 : GRID - 1 + P].rearrange("p (i j) -> p i j", j=GRID)
        from_right = wide[:, GRID + 1 : GRID + 1 + P].rearrange("p (i j) -> p i j", j=GRID)
        nc.vector.tensor_tensor(
            out=by_row[:, :, 1:GRID], in0=by_row[:, :, 1:GRID], in1=from_left[:, :, 1:GRID], op=ADD
        )
        nc.vector.tensor_tensor(
            out=by_row[:, :, 0 : GRID - 1],
            in0=by_row[:, :, 0 : GRID - 1],
            in1=from_right[:, :, 0 : GRID - 1],
            op=ADD,
        )

        acc = [acc_pool.tile([P, F_OUT], F32, name="acc%d" % r) for r in range(NODE_TILES)]
        bias = const.tile([P, F_OUT], BF16, name="bias")

        on_vector = [g for g in range(PASSES) if tensor_batches(g) < BATCH]
        x_pass = {}
        x_middle = {}
        w_pass = {}
        x_odd = {}
        grouped = {}
        codes = {}
        scales = {}

        def values(g):
            if g not in grouped:
                grouped[g] = regrouped.tile(
                    [P, NODES + F_OUT, PACK], BF16, name="mx_values", align_bytes=64
                )
            return grouped[g]

        def load(g):
            features = slice(g * K_PASS, (g + 1) * K_PASS)
            x_sb = loads.tile([P, NODE_TILES, K_PASS], BF16, name="x_sb")
            count = tensor_batches(g)
            for s in range(2):
                for view, first, end in ((x_halves, 0, count), (x_columns, count, BATCH)):
                    if first < end:
                        nc.sync.dma_start(
                            out=x_sb[:, 2 * s + first : 2 * s + end],
                            in_=view[s][:, first:end, features],
                        )
            x_pass[g] = x_sb
            if tensor_batches(g) > 0:
                x_mid = loads.tile([P, BATCH, K_PASS], BF16, name="x_mid")
                nc.sync.dma_start(
                    out=x_mid[:, 0 : tensor_batches(g)],
                    in_=X[0 : tensor_batches(g), MID_FIRST : MID_FIRST + P, features].rearrange("b p f -> p b f"),
                )
                x_middle[g] = x_mid
            w_sb = loads.tile([P, PACK, F_OUT], BF16, name="w_sb")
            nc.sync.dma_start(
                out=w_sb[:],
                in_=W_gcn[features, :].rearrange("(p t) o -> p t o", t=PACK),
            )
            w_pass[g] = w_sb

        def sum_tile(tiles, g):
            return tiles[on_vector.index(g) % SUM_TILES]

        def transpose_x(g):
            words = x_pass[g][:].bitcast(F32)
            batches = slice(tensor_batches(g), BATCH)
            for parity in range(2):
                xt = xt_pool.tile([P, BATCH, P, 2], F32, name="xt")
                for bb in range(tensor_batches(g), BATCH):
                    for u in range(2):
                        nc.tensor.transpose(
                            xt[:, bb, :, u], words[:, 2 * parity + bb, u : 2 * P : 2], ident[:]
                        )
                nodes = xt[:].rearrange("p b (i m) u -> p i b (m u)", i=GRID)[:, :, batches]
                if parity == 0:
                    even = sum_tile(even_tiles, g)[:, 1 : GRID + 1, batches, 0:HALF]
                    nc.scalar.copy(
                        out=even.rearrange("p i b m t -> p i b (m t)").bitcast(F32), in_=nodes
                    )
                else:
                    x_odd[g] = (
                        xt[:]
                        .rearrange("p b n u -> p (b n u)")
                        .bitcast(BF16)
                        .rearrange("p (b i m t) -> p i b m t", b=BATCH, i=GRID, t=PACK)[
                            :, :, batches
                        ]
                    )

        def sum_on_tensor(g):
            ax = values(g)[:, 0:NODES].rearrange("p (b n) t -> p b n t", b=BATCH)
            edge = P - GRID
            for bb in range(tensor_batches(g)):
                bank = xt_pool.tile([P, PACK, GRID * GRID], BF16, name="xt")
                for t in range(PACK):
                    x_up = x_pass[g][:, bb, t:K_PASS:PACK]
                    x_mid = x_middle[g][:, bb, t:K_PASS:PACK]
                    x_low = x_pass[g][:, 2 + bb, t:K_PASS:PACK]
                    for dst, lhsT, columns in (
                        (bank[:, t, 0:edge], x_up, adjacency[:, 0:edge]),
                        (bank[:, t, edge : P + GRID], x_mid, adjacency[:, 3 * GRID : 5 * GRID]),
                        (bank[:, t, P + GRID :], x_low, adjacency[:, GRID:P]),
                    ):
                        nc.tensor.matmul(out=dst, lhsT=lhsT, rhs=columns, start=True, stop=True)
                step = P if g == PASSES - 1 else GRID * GRID
                for n in range(0, GRID * GRID, step):
                    nc.scalar.copy(
                        out=ax[:, bb, n : n + step],
                        in_=bank[:, :, n : n + step].rearrange("p t n -> p n t"),
                    )

        def regroup_w(g):
            if regroup_on_pool(g):
                nc.gpsimd.tensor_scalar(
                    out=values(g)[:, NODES:],
                    in0=w_pass[g][:].rearrange("p t o -> p o t"),
                    scalar1=1.0,
                    scalar2=0.0,
                    op0=MULT,
                    op1=ADD,
                )
                return
            nc.scalar.copy(
                out=values(g)[:, NODES:].rearrange("p (c i) t -> p c t i", i=4),
                in_=w_pass[g][:].rearrange("p t (c i) -> p c t i", i=4),
            )

        def copy_single_terms(g):
            batches = slice(tensor_batches(g), BATCH)
            even = sum_tile(even_tiles, g)
            pair = sum_tile(pair_tiles, g)
            nc.scalar.copy(out=pair[:, 0, batches, 1:GRID:2], in_=even[:, 1, batches, 0:HALF])
            nc.scalar.copy(out=pair[:, GRID, batches, 2:GRID:2], in_=even[:, GRID, batches, 1:HALF])
            nc.scalar.copy(out=pair[:, 1:GRID, batches, 0], in_=even[:, 1:GRID, batches, 0])

        def add_pairs(g):
            batches = slice(tensor_batches(g), BATCH)
            even = sum_tile(even_tiles, g)
            pair = sum_tile(pair_tiles, g)
            nc.vector.tensor_tensor(
                out=pair[:, 0:GRID, batches, 2:SUMS:2],
                in0=x_odd[g],
                in1=even[:, 0:GRID, batches, 1 : HALF + 1],
                op=ADD,
            )
            nc.vector.tensor_tensor(
                out=pair[:, 1:SUMS, batches, 1:GRID:2],
                in0=x_odd[g],
                in1=even[:, 2 : GRID + 2, batches, 0:HALF],
                op=ADD,
            )

        def add_sums(engine, g, first, last):
            batches = slice(tensor_batches(g), BATCH)
            pair = sum_tile(pair_tiles, g)
            ax = values(g)[:, 0:NODES].rearrange("p (b i j) t -> p i b j t", b=BATCH, i=GRID)
            engine.tensor_tensor(
                out=ax[:, first:last, batches],
                in0=pair[:, first:last, batches, 0:GRID],
                in1=pair[:, first + 1 : last + 1, batches, 1:SUMS],
                op=ADD,
            )

        def quantise(g, first, last):
            if g not in codes:
                codes[g] = quant.tile([P, NODES + F_OUT], U32, name="mx_codes", align_bytes=64)
                scales[g] = quant.tile([P, NODES + F_OUT], U8, name="mx_scales", align_bytes=64)
            nc.vector.quantize_mx(
                out=codes[g][:, first:last].bitcast(FP8X4),
                scales=scales[g][:, first:last],
                in_=values(g)[:, first:last].rearrange("p n t -> p (n t)"),
            )

        def multiply(g, node_tiles=range(NODE_TILES)):
            for r in node_tiles:
                nodes = slice(r * P, (r + 1) * P)
                nc.tensor.matmul_mx(
                    out=acc[r][:],
                    lhsT=codes[g][:, nodes].bitcast(FP8X4),
                    lhsT_scale=scales[g][:, nodes],
                    rhs=codes[g][:, NODES:].bitcast(FP8X4),
                    rhs_scale=scales[g][:, NODES:],
                    start=(g == 0),
                    stop=(g == PASSES - 1),
                )

        def prepare(g):
            if g + LOADS_AHEAD < PASSES:
                load(g + LOADS_AHEAD)
            if tensor_batches(g) < BATCH:
                transpose_x(g)
            regroup_w(g)
            if tensor_batches(g) > 0:
                sum_on_tensor(g)
            if tensor_batches(g) < BATCH:
                copy_single_terms(g)

        with tc.manual_schedule():
            for g in range(LOADS_AHEAD):
                load(g)
            prepare(0)
            add_pairs(0)
            prepare(1)
            nc.sync.dma_start(out=bias[:], in_=b.partition_broadcast(P))
            prepared = 2
            quantised = 0
            multiplied = 0
            for k, g in enumerate(on_vector):
                following = on_vector[k + 1] if k + 1 < len(on_vector) else PASSES
                beside = BATCH - tensor_batches(following) if following < PASSES else 0
                pool_rows = POOL_ROWS * beside // BATCH
                if pool_rows > 0:
                    if k > 0:
                        zero_corner(sum_tile(pair_tiles, on_vector[k - 1]))
                    add_sums(nc.gpsimd, g, GRID - pool_rows, GRID)
                fresh = range(prepared, max(prepared, min(following + 3, PASSES)))
                for p in fresh:
                    if multiplied < quantised:
                        multiply(multiplied)
                        multiplied += 1
                    prepare(p)
                prepared = fresh.stop
                if following < PASSES:
                    add_pairs(following)
                for p in range(quantised, g - 1):
                    quantise(p, 0, NODES + F_OUT)
                add_sums(nc.vector, g, 0, GRID - pool_rows)
                for p in range(multiplied, quantised):
                    multiply(p)
                multiplied = quantised
                if g > 0:
                    quantise(g - 1, 0, NODES + F_OUT)
                quantised = g

            for p in range(quantised, PASSES - 1):
                quantise(p, 0, NODES + F_OUT)
            for p in range(multiplied, PASSES - 1):
                multiply(p)
            last = PASSES - 1
            quantise(last, NODES, NODES + F_OUT)
            for r in range(NODE_TILES):
                quantise(last, r * P, (r + 1) * P)
                multiply(last, range(r, r + 1))
            for r in range(NODE_TILES):
                result = results.tile([P, F_OUT], F32, name="result")
                nc.vector.tensor_tensor(out=result[:], in0=acc[r][:], in1=bias[:], op=ADD)
                nc.sync.dma_start(out=out_rows[r * P : (r + 1) * P, :], in_=result[:])
